import numpy as np
import ml_dtypes


def mxq(x, axis, fmt="e4m3"):
    dtype, down = {"e4m3": (ml_dtypes.float8_e4m3fn, 7), "e5m2": (ml_dtypes.float8_e5m2, 14)}[fmt]
    v = np.moveaxis(np.asarray(x, np.float32).astype(ml_dtypes.bfloat16).astype(np.float64), axis, -1)
    blocks = v.reshape(v.shape[:-1] + (-1, 32))
    amax = np.abs(blocks).max(-1, keepdims=True)
    byte = np.maximum(np.where(amax > 0, np.frexp(amax)[1] - 1 + 127, 0) - down, 1)
    scale = np.exp2(byte - 127.0)
    codes = (blocks / scale).astype(np.float32).astype(dtype).astype(np.float64)
    return np.moveaxis((codes * scale).reshape(v.shape), -1, axis)


WIDE = False


def mx_kscale(k):
    if not WIDE:
        return np.ones(k)
    levels = np.array([10, -10, 5, -5, 0])
    a = np.random.permutation(np.resize(levels, k // 512 * 4)).reshape(k // 512, 4)
    idx = np.arange(k)
    return np.exp2(a[idx // 512, idx % 128 // 32])


BF16 = ml_dtypes.bfloat16


def bf(x):
    return np.asarray(x, np.float32).astype(BF16)


def f64(x):
    return np.asarray(x).astype(np.float64)


N, M, MOL, PROT, F, D = 1024, 2048, 768, 1280, 1024, 1024
EPS = 1e-8


def l2_normalise(v):
    return v / np.maximum(np.sqrt((v * v).sum(-1, keepdims=True)), EPS)


def setup_inputs():
    s, t = mx_kscale(F), mx_kscale(F)
    return {
        "h_mol": bf(np.maximum(np.random.standard_normal((N, F)), 0.0) * s),
        "h_prot": bf(np.maximum(np.random.standard_normal((M, F)), 0.0) * t),
        "Wm2": bf(np.random.standard_normal((D, F)) / np.sqrt(F) / s),
        "bm2": bf(np.random.standard_normal(D) * 0.2),
        "Wp2": bf(np.random.standard_normal((D, F)) / np.sqrt(F) / t),
        "bp2": bf(np.random.standard_normal(D) * 0.2),
        "temperature": bf(0.1 * (1.0 + 0.1 * np.random.standard_normal(1))),
    }


def reference(h_mol, h_prot, Wm2, bm2, Wp2, bp2, temperature):
    mp = (mxq(f64(h_mol), 1, "e4m3") @ mxq(f64(Wm2), 1, "e4m3").T) + f64(bm2)
    pp = (mxq(f64(h_prot), 1, "e4m3") @ mxq(f64(Wp2), 1, "e4m3").T) + f64(bp2)
    mn = l2_normalise(mp)
    pn = l2_normalise(pp)
    distance = mxq(pn, 1, "e4m3") @ mxq(mn, 1, "e4m3").T
    return distance / f64(temperature)

@@ -1,0 +1,248 @@
+from contextlib import ExitStack
+
+import concourse.masks as masks
+import concourse.mybir as mybir
+
+F32 = mybir.dt.float32
+BF16 = mybir.dt.bfloat16
+U32 = mybir.dt.uint32
+U8 = mybir.dt.uint8
+FP8X4 = mybir.dt.float8_e4m3fn_x4
+ACT = mybir.ActivationFunctionType
+ALU = mybir.AluOpType
+
+P = 128
+N_MOL, N_PROT, F, D = 1024, 2048, 1024, 1024
+EPS = 1e-8
+FLOPS = 2 * (N_MOL * F * D + N_PROT * F * D + N_PROT * N_MOL * D)
+
+PINNED = True
+
+
+def tile_coembedding_pa_kernel(tc, h_mol, h_prot, Wm2, bm2, Wp2, bp2, temperature, out):
+    nc = tc.nc
+    with ExitStack() as ctx:
+        keep = ctx.enter_context(tc.tile_pool(name="keep", bufs=1))
+        rawp = ctx.enter_context(tc.tile_pool(name="rawp", bufs=6))
+        grpp = ctx.enter_context(tc.tile_pool(name="grpp", bufs=3))
+        yp = ctx.enter_context(tc.tile_pool(name="yp", bufs=6))
+        wrk = ctx.enter_context(tc.tile_pool(name="wrk", bufs=3))
+        psum = ctx.enter_context(tc.psum_pool(name="psum", bufs=8))
+        if PINNED:
+            ctx.enter_context(tc.manual_schedule())
+
+        brow = keep.tile([P, 2 * D], BF16, name="brow", tag="brow")
+        nc.vector.memset(brow[:], 0.0)
+        nc.scalar.dma_start(out=brow[0:1, 0:D], in_=bm2.rearrange("(o n) -> o n", o=1))
+        nc.scalar.dma_start(out=brow[0:1, D:2 * D], in_=bp2.rearrange("(o n) -> o n", o=1))
+        t_bf = keep.tile([P, 1], BF16, name="t_bf", tag="t_bf")
+        nc.scalar.dma_start(out=t_bf[:], in_=temperature.partition_broadcast(P))
+        warm = keep.tile([P, 1], F32, name="warm", tag="warm")
+        nc.vector.memset(warm[:], 1.0)
+        nc.scalar.sqrt(warm[:], warm[:])
+        ident_f = keep.tile([P, P], F32, name="ident_f", tag="ident_f")
+        masks.make_identity(nc, ident_f[:])
+        ident_b = keep.tile([P, P], BF16, name="ident_b", tag="ident_b")
+        masks.make_identity(nc, ident_b[:])
+        ones_b = keep.tile([P, P], BF16, name="ones_b", tag="ones_b")
+        nc.vector.memset(ones_b[:], 1.0)
+
+        def codes_and_scales(label, shape):
+            c = keep.tile(shape, U32, name=label + "_c", tag=label + "_c", align_bytes=64)
+            s = keep.tile(shape, U8, name=label + "_s", tag=label + "_s", align_bytes=64)
+            return c, s
+
+        wm_c, wm_s = codes_and_scales("wm", [P, 2, D])
+        wp_c, wp_s = codes_and_scales("wp", [P, 2, D])
+        hm_c, hm_s = codes_and_scales("hm", [P, 2, N_MOL])
+        hp_c, hp_s = codes_and_scales("hp", [P, 2, N_PROT])
+        mn_c, mn_s = codes_and_scales("mn", [P, 2, N_MOL])
+        pn_c, pn_s = codes_and_scales("pn", [P, N_PROT // P, 2 * P])
+
+        def w_rows(w, c):
+            return w.rearrange("(c r j) f -> c r j f", c=2, r=P, j=4)[c]
+
+        def h_rows(h, g):
+            return h[g * 512:(g + 1) * 512, :].rearrange("(t r) f -> r t f", t=4)
+
+        groups = [
+            (w_rows(Wm2, 0), wm_c, wm_s, 0),
+            (w_rows(Wm2, 1), wm_c, wm_s, 512),
+            (h_rows(h_mol, 0), hm_c, hm_s, 0),
+            (h_rows(h_mol, 1), hm_c, hm_s, 512),
+            (w_rows(Wp2, 0), wp_c, wp_s, 0),
+            (w_rows(Wp2, 1), wp_c, wp_s, 512),
+            (h_rows(h_prot, 0), hp_c, hp_s, 0),
+            (h_rows(h_prot, 1), hp_c, hp_s, 512),
+            (h_rows(h_prot, 2), hp_c, hp_s, 1024),
+            (h_rows(h_prot, 3), hp_c, hp_s, 1536),
+        ]
+        raws, grps = {}, {}
+
+        def load(gi):
+            raw = rawp.tile([P, 4, F], BF16, name="raw", tag="raw")
+            nc.sync.dma_start(out=raw[:], in_=groups[gi][0])
+            raws[gi] = raw
+
+        def in_block(gi):
+            rawf = raws[gi][:].rearrange("p t f -> p (t f)").bitcast(F32)
+            grp = grpp.tile([P, 4096], BF16, name="grp", tag="grp", align_bytes=64)
+            grpw = grp[:].bitcast(F32).rearrange("q (g n u) -> q g n u", g=2, n=512, u=2)
+            for t in range(4):
+                tin = psum.tile([P, 4, P], F32, name="tin", tag="bank")
+                for gu in range(4):
+                    lo = t * 512 + gu * P
+                    nc.tensor.transpose(tin[:, gu, :], rawf[:, lo:lo + P], ident_f[:])
+                src = tin[:].rearrange("q (g u) r -> q g r u", g=2, u=2)
+                dst = grpw[:, :, t * P:(t + 1) * P, :]
+                if t == 3:
+                    nc.vector.tensor_copy(out=dst, in_=src)
+                else:
+                    nc.scalar.copy(out=dst, in_=src)
+            grps[gi] = grp
+            if gi + 6 < len(groups):
+                load(gi + 6)
+
+        def q_block(gi):
+            codes, scales, col0 = groups[gi][1], groups[gi][2], groups[gi][3]
+            for g in range(2):
+                nc.vector.quantize_mx(
+                    out=codes[:, g, col0:col0 + 512].bitcast(FP8X4),
+                    scales=scales[:, g, col0:col0 + 512],
+                    in_=grps[gi][:, g * 2048:(g + 1) * 2048],
+                )
+
+        for gi in range(6):
+            load(gi)
+
+        biases = []
+
+        def bias_block(b):
+            bias = keep.tile([P, D], F32, name="bias%d" % b, tag="bias%d" % b)
+            for c in range(2):
+                bb = psum.tile([P, 512], F32, name="bb", tag="bank")
+                lo = b * D + c * 512
+                nc.tensor.matmul(bb[:], lhsT=ones_b[:], rhs=brow[:, lo:lo + 512], start=True, stop=True)
+                nc.vector.tensor_copy(
+                    out=bias[:, c * 512:(c + 1) * 512].rearrange("p (j r) -> p j r", j=4),
+                    in_=bb[:].rearrange("p (r j) -> p j r", j=4),
+                )
+            biases.append(bias)
+
+        t_f = keep.tile([P, 1], F32, name="t_f", tag="t_f")
+        nc.vector.tensor_copy(out=t_f[:], in_=t_bf[:])
+        inv_t = keep.tile([P, 1], F32, name="inv_t", tag="inv_t")
+        nc.vector.reciprocal(out=inv_t[:], in_=t_f[:])
+
+        ys, rs, sss = {}, {}, {}
+
+        def operands(i):
+            if i < 8:
+                return hm_c, hm_s, wm_c, wm_s, biases[0], i
+            return hp_c, hp_s, wp_c, wp_s, biases[1], i - 8
+
+        def a_block(k):
+            ss = wrk.tile([P, 2], F32, name="ss", tag="ss", bufs=4)
+            for e in range(2):
+                i = 2 * k + e
+                hc, hs, wc, ws, bias, rt = operands(i)
+                y = yp.tile([P, D], F32, name="y", tag="y")
+                ys[i] = y
+                for c in range(2):
+                    x = psum.tile([P, 512], F32, name="x", tag="bank")
+                    for g in range(2):
+                        nc.tensor.matmul_mx(
+                            out=x[:],
+                            lhsT=hc[:, g, rt * P:(rt + 1) * P].bitcast(FP8X4),
+                            lhsT_scale=hs[:, g, rt * P:(rt + 1) * P],
+                            rhs=wc[:, g, c * 512:(c + 1) * 512].bitcast(FP8X4),
+                            rhs_scale=ws[:, g, c * 512:(c + 1) * 512],
+                            start=(g == 0),
+                            stop=(g == 1),
+                        )
+                    nc.vector.tensor_tensor(
+                        out=y[:, c * 512:(c + 1) * 512], in0=x[:], in1=bias[:, c * 512:(c + 1) * 512], op=ALU.add
+                    )
+                junk = wrk.tile([P, D], BF16, name="junk", tag="junk", bufs=2)
+                nc.scalar.activation(out=junk[:], in_=y[:], func=ACT.Square, accum_out=ss[:, e:e + 1])
+            nrm = wrk.tile([P, 2], F32, name="nrm", tag="nrm", bufs=4)
+            nc.scalar.sqrt(nrm[:], ss[:])
+            sss[k] = nrm
+
+        def n_block(k):
+            nrm = sss[k]
+            r = wrk.tile([P, 2], F32, name="r", tag="r", bufs=4)
+            nc.vector.tensor_scalar_max(out=r[:], in0=nrm[:], scalar1=EPS)
+            nc.vector.reciprocal(out=r[:], in_=r[:])
+            for e in range(2):
+                i = 2 * k + e
+                z = wrk.tile([P, D], BF16, name="z", tag="z", bufs=6)
+                nc.gpsimd.tensor_scalar(
+                    out=z[:], in0=ys[i][:], scalar1=r[:, e:e + 1], scalar2=0.0, op0=ALU.mult, op1=ALU.add
+                )
+                rs[i] = z
+
+        def b_block(k):
+            g2s = []
+            for e in range(2):
+                i = 2 * k + e
+                z = rs[i]
+                t2 = psum.tile([P, 8, P], BF16, name="t2", tag="bank")
+                for tau in range(8):
+                    nc.tensor.transpose(t2[:, tau, :], z[:, tau * P:(tau + 1) * P], ident_b[:])
+                g2 = wrk.tile([P, D], BF16, name="g2", tag="g2", bufs=4, align_bytes=64)
+                g2s.append(g2)
+                dst = g2[:].rearrange("p (c m j) -> p c m j", c=2, m=P, j=4)
+                src = t2[:].rearrange("p (c j) m -> p c m j", c=2, j=4)
+                if i % 4 == 3:
+                    nc.scalar.copy(out=dst, in_=src)
+                else:
+                    nc.vector.tensor_copy(out=dst, in_=src)
+            for e in range(2):
+                i = 2 * k + e
+                g2 = g2s[e]
+                if i < 8:
+                    for c in range(2):
+                        nc.vector.quantize_mx(
+                            out=mn_c[:, c, i * P:(i + 1) * P].bitcast(FP8X4),
+                            scales=mn_s[:, c, i * P:(i + 1) * P],
+                            in_=g2[:, c * 512:(c + 1) * 512],
+                        )
+                else:
+                    nc.vector.quantize_mx(
+                        out=pn_c[:, i - 8, :].bitcast(FP8X4), scales=pn_s[:, i - 8, :], in_=g2[:]
+                    )
+
+        def c_block(k):
+            for e in range(2):
+                rt = 2 * k + e - 8
+                osb = wrk.tile([P, N_MOL], F32, name="osb", tag="osb", bufs=3)
+                for nh in range(2):
+                    o = psum.tile([P, 512], F32, name="o", tag="bank")
+                    for c in range(2):
+                        nc.tensor.matmul_mx(
+                            out=o[:],
+                            lhsT=pn_c[:, rt, c * P:(c + 1) * P].bitcast(FP8X4),
+                            lhsT_scale=pn_s[:, rt, c * P:(c + 1) * P],
+                            rhs=mn_c[:, c, nh * 512:(nh + 1) * 512].bitcast(FP8X4),
+                            rhs_scale=mn_s[:, c, nh * 512:(nh + 1) * 512],
+                            start=(c == 0),
+                            stop=(c == 1),
+                        )
+                    nc.scalar.activation(
+                        out=osb[:, nh * 512:(nh + 1) * 512], in_=o[:], func=ACT.Copy, scale=inv_t[:, 0:1]
+                    )
+                nc.sync.dma_start(out=out[rt * P:(rt + 1) * P, :], in_=osb[:])
+
+        seq = [
+            ("I", 0), ("I", 1), ("Q", 0), ("I", 2), ("Q", 1), ("S", 0), ("S", 1), ("Q", 2), ("A", 0), ("A", 1),
+            ("I", 3), ("N", 0), ("Q", 3), ("A", 2), ("N", 1), ("B", 0), ("A", 3), ("N", 2), ("I", 4), ("B", 1),
+            ("N", 3), ("Q", 4), ("I", 5), ("B", 2), ("Q", 5), ("I", 6), ("B", 3), ("Q", 6), ("A", 4), ("I", 7),
+            ("A", 5), ("N", 4), ("Q", 7), ("A", 6), ("N", 5), ("B", 4), ("I", 8), ("A", 7), ("N", 6), ("Q", 8),
+            ("B", 5), ("C", 4), ("A", 8), ("N", 7), ("B", 6), ("C", 5), ("I", 9), ("A", 9), ("N", 8), ("Q", 9),
+            ("B", 7), ("C", 6), ("A", 10), ("N", 9), ("B", 8), ("C", 7), ("A", 11), ("N", 10), ("B", 9), ("C", 8),
+            ("N", 11), ("B", 10), ("C", 9), ("B", 11), ("C", 10), ("C", 11),
+        ]
+        kinds = {"I": in_block, "Q": q_block, "S": bias_block, "A": a_block, "N": n_block, "B": b_block, "C": c_block}
+        for step in seq:
+            kinds[step[0]](step[1])

@@ -95,7 +95,7 @@ def tile_coembedding_pa_kernel(tc, h_mol, h_prot, Wm2, bm2, Wp2, bp2, temperatur
                     nc.tensor.transpose(tin[:, gu, :], rawf[:, lo:lo + P], ident_f[:])
                 src = tin[:].rearrange("q (g u) r -> q g r u", g=2, u=2)
                 dst = grpw[:, :, t * P:(t + 1) * P, :]
-                if t == 3:
+                if gi < 3 and t % 2 == 1:
                     nc.vector.tensor_copy(out=dst, in_=src)
                 else:
                     nc.scalar.copy(out=dst, in_=src)
@@ -115,7 +115,7 @@ def tile_coembedding_pa_kernel(tc, h_mol, h_prot, Wm2, bm2, Wp2, bp2, temperatur
         for gi in range(6):
             load(gi)
 
-        biases = []
+        biases = {}
 
         def bias_block(b):
             bias = keep.tile([P, D], F32, name="bias%d" % b, tag="bias%d" % b)
@@ -127,14 +127,14 @@ def tile_coembedding_pa_kernel(tc, h_mol, h_prot, Wm2, bm2, Wp2, bp2, temperatur
                     out=bias[:, c * 512:(c + 1) * 512].rearrange("p (j r) -> p j r", j=4),
                     in_=bb[:].rearrange("p (r j) -> p j r", j=4),
                 )
-            biases.append(bias)
+            biases[b] = bias
 
         t_f = keep.tile([P, 1], F32, name="t_f", tag="t_f")
         nc.vector.tensor_copy(out=t_f[:], in_=t_bf[:])
         inv_t = keep.tile([P, 1], F32, name="inv_t", tag="inv_t")
         nc.vector.reciprocal(out=inv_t[:], in_=t_f[:])
 
-        ys, rs, sss = {}, {}, {}
+        ys, rs, sss, g2s = {}, {}, {}, {}
 
         def operands(i):
             if i < 8:
@@ -142,7 +142,6 @@ def tile_coembedding_pa_kernel(tc, h_mol, h_prot, Wm2, bm2, Wp2, bp2, temperatur
             return hp_c, hp_s, wp_c, wp_s, biases[1], i - 8
 
         def a_block(k):
-            ss = wrk.tile([P, 2], F32, name="ss", tag="ss", bufs=4)
             for e in range(2):
                 i = 2 * k + e
                 hc, hs, wc, ws, bias, rt = operands(i)
@@ -163,8 +162,12 @@ def tile_coembedding_pa_kernel(tc, h_mol, h_prot, Wm2, bm2, Wp2, bp2, temperatur
                     nc.vector.tensor_tensor(
                         out=y[:, c * 512:(c + 1) * 512], in0=x[:], in1=bias[:, c * 512:(c + 1) * 512], op=ALU.add
                     )
-                junk = wrk.tile([P, D], BF16, name="junk", tag="junk", bufs=2)
-                nc.scalar.activation(out=junk[:], in_=y[:], func=ACT.Square, accum_out=ss[:, e:e + 1])
+
+        def w_block(k):
+            ss = wrk.tile([P, 2], F32, name="ss", tag="ss", bufs=4)
+            for e in range(2):
+                junk = wrk.tile([P, D], BF16, name="junk", tag="junk", bufs=1)
+                nc.scalar.activation(out=junk[:], in_=ys[2 * k + e][:], func=ACT.Square, accum_out=ss[:, e:e + 1])
             nrm = wrk.tile([P, 2], F32, name="nrm", tag="nrm", bufs=4)
             nc.scalar.sqrt(nrm[:], ss[:])
             sss[k] = nrm
@@ -183,7 +186,6 @@ def tile_coembedding_pa_kernel(tc, h_mol, h_prot, Wm2, bm2, Wp2, bp2, temperatur
                 rs[i] = z
 
         def b_block(k):
-            g2s = []
             for e in range(2):
                 i = 2 * k + e
                 z = rs[i]
@@ -191,32 +193,30 @@ def tile_coembedding_pa_kernel(tc, h_mol, h_prot, Wm2, bm2, Wp2, bp2, temperatur
                 for tau in range(8):
                     nc.tensor.transpose(t2[:, tau, :], z[:, tau * P:(tau + 1) * P], ident_b[:])
                 g2 = wrk.tile([P, D], BF16, name="g2", tag="g2", bufs=4, align_bytes=64)
-                g2s.append(g2)
+                g2s[i] = g2
                 dst = g2[:].rearrange("p (c m j) -> p c m j", c=2, m=P, j=4)
                 src = t2[:].rearrange("p (c j) m -> p c m j", c=2, j=4)
-                if i % 4 == 3:
+                if i % 2 == 1 and i < 8:
                     nc.scalar.copy(out=dst, in_=src)
                 else:
                     nc.vector.tensor_copy(out=dst, in_=src)
-            for e in range(2):
-                i = 2 * k + e
-                g2 = g2s[e]
-                if i < 8:
-                    for c in range(2):
-                        nc.vector.quantize_mx(
-                            out=mn_c[:, c, i * P:(i + 1) * P].bitcast(FP8X4),
-                            scales=mn_s[:, c, i * P:(i + 1) * P],
-                            in_=g2[:, c * 512:(c + 1) * 512],
-                        )
-                else:
+
+        def r_block(i):
+            g2 = g2s[i]
+            if i < 8:
+                for c in range(2):
                     nc.vector.quantize_mx(
-                        out=pn_c[:, i - 8, :].bitcast(FP8X4), scales=pn_s[:, i - 8, :], in_=g2[:]
+                        out=mn_c[:, c, i * P:(i + 1) * P].bitcast(FP8X4),
+                        scales=mn_s[:, c, i * P:(i + 1) * P],
+                        in_=g2[:, c * 512:(c + 1) * 512],
                     )
+            else:
+                nc.vector.quantize_mx(out=pn_c[:, i - 8, :].bitcast(FP8X4), scales=pn_s[:, i - 8, :], in_=g2[:])
 
         def c_block(k):
             for e in range(2):
                 rt = 2 * k + e - 8
-                osb = wrk.tile([P, N_MOL], F32, name="osb", tag="osb", bufs=3)
+                osb = wrk.tile([P, N_MOL], F32, name="osb", tag="osb", bufs=4)
                 for nh in range(2):
                     o = psum.tile([P, 512], F32, name="o", tag="bank")
                     for c in range(2):
@@ -229,20 +229,30 @@ def tile_coembedding_pa_kernel(tc, h_mol, h_prot, Wm2, bm2, Wp2, bp2, temperatur
                             start=(c == 0),
                             stop=(c == 1),
                         )
-                    nc.scalar.activation(
-                        out=osb[:, nh * 512:(nh + 1) * 512], in_=o[:], func=ACT.Copy, scale=inv_t[:, 0:1]
-                    )
+                    if rt >= 12 and nh == 1:
+                        nc.vector.tensor_scalar_mul(out=osb[:, nh * 512:(nh + 1) * 512], in0=o[:], scalar1=inv_t[:, 0:1])
+                    else:
+                        nc.scalar.activation(
+                            out=osb[:, nh * 512:(nh + 1) * 512], in_=o[:], func=ACT.Copy, scale=inv_t[:, 0:1]
+                        )
                 nc.sync.dma_start(out=out[rt * P:(rt + 1) * P, :], in_=osb[:])
 
         seq = [
-            ("I", 0), ("I", 1), ("Q", 0), ("I", 2), ("Q", 1), ("S", 0), ("S", 1), ("Q", 2), ("A", 0), ("A", 1),
-            ("I", 3), ("N", 0), ("Q", 3), ("A", 2), ("N", 1), ("B", 0), ("A", 3), ("N", 2), ("I", 4), ("B", 1),
-            ("N", 3), ("Q", 4), ("I", 5), ("B", 2), ("Q", 5), ("I", 6), ("B", 3), ("Q", 6), ("A", 4), ("I", 7),
-            ("A", 5), ("N", 4), ("Q", 7), ("A", 6), ("N", 5), ("B", 4), ("I", 8), ("A", 7), ("N", 6), ("Q", 8),
-            ("B", 5), ("C", 4), ("A", 8), ("N", 7), ("B", 6), ("C", 5), ("I", 9), ("A", 9), ("N", 8), ("Q", 9),
-            ("B", 7), ("C", 6), ("A", 10), ("N", 9), ("B", 8), ("C", 7), ("A", 11), ("N", 10), ("B", 9), ("C", 8),
-            ("N", 11), ("B", 10), ("C", 9), ("B", 11), ("C", 10), ("C", 11),
+            ("S", 1), ("S", 0), ("I", 0), ("Q", 0), ("I", 1), ("Q", 1), ("I", 2), ("I", 3), ("Q", 2), ("A", 0),
+            ("W", 0), ("Q", 3), ("I", 4), ("A", 1), ("W", 1), ("N", 0), ("A", 2), ("Q", 4), ("N", 1), ("I", 6),
+            ("I", 5), ("A", 3), ("W", 2), ("B", 0), ("Q", 6), ("Q", 5), ("I", 7), ("N", 2), ("A", 4), ("W", 3),
+            ("B", 1), ("r", 0), ("r", 2), ("Q", 7), ("r", 1), ("A", 5), ("N", 3), ("W", 4), ("r", 3), ("B", 2),
+            ("r", 4), ("N", 4), ("A", 6), ("I", 8), ("r", 5), ("W", 5), ("B", 3), ("B", 4), ("r", 8), ("Q", 8),
+            ("W", 6), ("I", 9), ("r", 7), ("N", 5), ("r", 9), ("A", 7), ("r", 6), ("N", 6), ("A", 8), ("C", 4),
+            ("Q", 9), ("B", 5), ("r", 10), ("W", 7), ("W", 8), ("r", 11), ("N", 7), ("B", 6), ("A", 9), ("C", 5),
+            ("r", 13), ("r", 12), ("N", 8), ("B", 7), ("W", 9), ("r", 14), ("A", 10), ("C", 6), ("r", 15), ("N", 9),
+            ("W", 10), ("B", 8), ("r", 17), ("C", 7), ("r", 16), ("N", 10), ("A", 11), ("W", 11), ("B", 9), ("C", 8),
+            ("r", 18), ("r", 19), ("N", 11), ("B", 10), ("r", 20), ("r", 21), ("C", 9), ("B", 11), ("r", 22), ("C", 10),
+            ("r", 23), ("C", 11),
         ]
-        kinds = {"I": in_block, "Q": q_block, "S": bias_block, "A": a_block, "N": n_block, "B": b_block, "C": c_block}
+        kinds = {
+            "I": in_block, "Q": q_block, "S": bias_block, "A": a_block, "W": w_block, "N": n_block,
+            "B": b_block, "r": r_block, "C": c_block,
+        }
         for step in seq:
             kinds[step[0]](step[1])

@@ -16,41 +16,27 @@ N_MOL, N_PROT, F, D = 1024, 2048, 1024, 1024
 EPS = 1e-8
 FLOPS = 2 * (N_MOL * F * D + N_PROT * F * D + N_PROT * N_MOL * D)
 
-PINNED = True
+BANK = 512
+GROUP = 4 * P
+MOL_TILES = N_MOL // P
+TILES = (N_MOL + N_PROT) // P
+PAIRS = TILES // 2
+MOL_PAIRS = MOL_TILES // 2
+RAW_BUFS = 6
 
 
 def tile_coembedding_pa_kernel(tc, h_mol, h_prot, Wm2, bm2, Wp2, bp2, temperature, out):
     nc = tc.nc
     with ExitStack() as ctx:
         keep = ctx.enter_context(tc.tile_pool(name="keep", bufs=1))
-        rawp = ctx.enter_context(tc.tile_pool(name="rawp", bufs=6))
-        grpp = ctx.enter_context(tc.tile_pool(name="grpp", bufs=3))
-        yp = ctx.enter_context(tc.tile_pool(name="yp", bufs=6))
-        wrk = ctx.enter_context(tc.tile_pool(name="wrk", bufs=3))
+        work = ctx.enter_context(tc.tile_pool(name="work", bufs=1))
         psum = ctx.enter_context(tc.psum_pool(name="psum", bufs=8))
-        if PINNED:
-            ctx.enter_context(tc.manual_schedule())
-
-        brow = keep.tile([P, 2 * D], BF16, name="brow", tag="brow")
-        nc.vector.memset(brow[:], 0.0)
-        nc.scalar.dma_start(out=brow[0:1, 0:D], in_=bm2.rearrange("(o n) -> o n", o=1))
-        nc.scalar.dma_start(out=brow[0:1, D:2 * D], in_=bp2.rearrange("(o n) -> o n", o=1))
-        t_bf = keep.tile([P, 1], BF16, name="t_bf", tag="t_bf")
-        nc.scalar.dma_start(out=t_bf[:], in_=temperature.partition_broadcast(P))
-        warm = keep.tile([P, 1], F32, name="warm", tag="warm")
-        nc.vector.memset(warm[:], 1.0)
-        nc.scalar.sqrt(warm[:], warm[:])
-        ident_f = keep.tile([P, P], F32, name="ident_f", tag="ident_f")
-        masks.make_identity(nc, ident_f[:])
-        ident_b = keep.tile([P, P], BF16, name="ident_b", tag="ident_b")
-        masks.make_identity(nc, ident_b[:])
-        ones_b = keep.tile([P, P], BF16, name="ones_b", tag="ones_b")
-        nc.vector.memset(ones_b[:], 1.0)
+        ctx.enter_context(tc.manual_schedule())
 
         def codes_and_scales(label, shape):
-            c = keep.tile(shape, U32, name=label + "_c", tag=label + "_c", align_bytes=64)
-            s = keep.tile(shape, U8, name=label + "_s", tag=label + "_s", align_bytes=64)
-            return c, s
+            codes = keep.tile(shape, U32, name=label + "_c", tag=label + "_c", align_bytes=64)
+            scales = keep.tile(shape, U8, name=label + "_s", tag=label + "_s", align_bytes=64)
+            return codes, scales
 
         wm_c, wm_s = codes_and_scales("wm", [P, 2, D])
         wp_c, wp_s = codes_and_scales("wp", [P, 2, D])
@@ -63,196 +49,209 @@ def tile_coembedding_pa_kernel(tc, h_mol, h_prot, Wm2, bm2, Wp2, bp2, temperatur
             return w.rearrange("(c r j) f -> c r j f", c=2, r=P, j=4)[c]
 
         def h_rows(h, g):
-            return h[g * 512:(g + 1) * 512, :].rearrange("(t r) f -> r t f", t=4)
+            return h[g * GROUP:(g + 1) * GROUP, :].rearrange("(t r) f -> r t f", t=4)
 
         groups = [
             (w_rows(Wm2, 0), wm_c, wm_s, 0),
-            (w_rows(Wm2, 1), wm_c, wm_s, 512),
+            (w_rows(Wm2, 1), wm_c, wm_s, GROUP),
             (h_rows(h_mol, 0), hm_c, hm_s, 0),
-            (h_rows(h_mol, 1), hm_c, hm_s, 512),
+            (h_rows(h_mol, 1), hm_c, hm_s, GROUP),
             (w_rows(Wp2, 0), wp_c, wp_s, 0),
-            (w_rows(Wp2, 1), wp_c, wp_s, 512),
+            (w_rows(Wp2, 1), wp_c, wp_s, GROUP),
             (h_rows(h_prot, 0), hp_c, hp_s, 0),
-            (h_rows(h_prot, 1), hp_c, hp_s, 512),
-            (h_rows(h_prot, 2), hp_c, hp_s, 1024),
-            (h_rows(h_prot, 3), hp_c, hp_s, 1536),
+            (h_rows(h_prot, 1), hp_c, hp_s, GROUP),
+            (h_rows(h_prot, 2), hp_c, hp_s, 2 * GROUP),
+            (h_rows(h_prot, 3), hp_c, hp_s, 3 * GROUP),
         ]
-        raws, grps = {}, {}
+        raws, grouped, biases, ys, norms, zs, regrouped = {}, {}, {}, {}, {}, {}, {}
 
-        def load(gi):
-            raw = rawp.tile([P, 4, F], BF16, name="raw", tag="raw")
-            nc.sync.dma_start(out=raw[:], in_=groups[gi][0])
-            raws[gi] = raw
+        def load(g):
+            raws[g] = work.tile([P, 4, F], BF16, name="raw", tag="raw", bufs=RAW_BUFS)
+            nc.sync.dma_start(out=raws[g][:], in_=groups[g][0])
 
-        def in_block(gi):
-            rawf = raws[gi][:].rearrange("p t f -> p (t f)").bitcast(F32)
-            grp = grpp.tile([P, 4096], BF16, name="grp", tag="grp", align_bytes=64)
-            grpw = grp[:].bitcast(F32).rearrange("q (g n u) -> q g n u", g=2, n=512, u=2)
+        brow = keep.tile([P, 2 * D], BF16, name="brow", tag="brow")
+        nc.vector.memset(brow[:], 0.0)
+        t_bf = keep.tile([P, 1], BF16, name="t_bf", tag="t_bf")
+        nc.scalar.dma_start(out=t_bf[:], in_=temperature.partition_broadcast(P))
+        load(0)
+        nc.sync.dma_start(out=brow[0:1, 0:D], in_=bm2.rearrange("(o n) -> o n", o=1))
+        nc.sync.dma_start(out=brow[0:1, D:2 * D], in_=bp2.rearrange("(o n) -> o n", o=1))
+        for g in range(1, RAW_BUFS):
+            load(g)
+        warm = keep.tile([P, 1], F32, name="warm", tag="warm")
+        nc.vector.memset(warm[:], 1.0)
+        nc.scalar.sqrt(warm[:], warm[:])
+        ident_f = keep.tile([P, P], F32, name="ident_f", tag="ident_f")
+        masks.make_identity(nc, ident_f[:])
+        ident_b = keep.tile([P, P], BF16, name="ident_b", tag="ident_b")
+        masks.make_identity(nc, ident_b[:])
+        ones_b = keep.tile([P, P], BF16, name="ones_b", tag="ones_b")
+        nc.vector.memset(ones_b[:], 1.0)
+        t_f = keep.tile([P, 1], F32, name="t_f", tag="t_f")
+        inv_t = keep.tile([P, 1], F32, name="inv_t", tag="inv_t")
+
+        def temperature_reciprocal():
+            nc.vector.tensor_copy(out=t_f[:], in_=t_bf[:])
+            nc.vector.reciprocal(out=inv_t[:], in_=t_f[:])
+
+        def transpose_group(g):
+            words = raws[g][:].rearrange("p t f -> p (t f)").bitcast(F32)
+            grp = work.tile([P, 4 * 2 * BANK], BF16, name="grp", tag="grp", bufs=3, align_bytes=64)
+            grouped[g] = grp
+            grp_words = grp[:].bitcast(F32).rearrange("q (g n u) -> q g n u", g=2, n=GROUP, u=2)
             for t in range(4):
-                tin = psum.tile([P, 4, P], F32, name="tin", tag="bank")
+                bank = psum.tile([P, 4, P], F32, name="tin", tag="bank")
                 for gu in range(4):
-                    lo = t * 512 + gu * P
-                    nc.tensor.transpose(tin[:, gu, :], rawf[:, lo:lo + P], ident_f[:])
-                src = tin[:].rearrange("q (g u) r -> q g r u", g=2, u=2)
-                dst = grpw[:, :, t * P:(t + 1) * P, :]
-                if gi < 3 and t % 2 == 1:
+                    lo = t * BANK + gu * P
+                    nc.tensor.transpose(bank[:, gu, :], words[:, lo:lo + P], ident_f[:])
+                src = bank[:].rearrange("q (g u) r -> q g r u", g=2, u=2)
+                dst = grp_words[:, :, t * P:(t + 1) * P, :]
+                if (g < 3 and t % 2 == 1) or (3 <= g < 6 and t == 3):
                     nc.vector.tensor_copy(out=dst, in_=src)
                 else:
                     nc.scalar.copy(out=dst, in_=src)
-            grps[gi] = grp
-            if gi + 6 < len(groups):
-                load(gi + 6)
+            if g + RAW_BUFS < len(groups):
+                load(g + RAW_BUFS)
 
-        def q_block(gi):
-            codes, scales, col0 = groups[gi][1], groups[gi][2], groups[gi][3]
-            for g in range(2):
+        def quantise_group(g):
+            codes, scales, col0 = groups[g][1], groups[g][2], groups[g][3]
+            for p in range(2):
                 nc.vector.quantize_mx(
-                    out=codes[:, g, col0:col0 + 512].bitcast(FP8X4),
-                    scales=scales[:, g, col0:col0 + 512],
-                    in_=grps[gi][:, g * 2048:(g + 1) * 2048],
+                    out=codes[:, p, col0:col0 + GROUP].bitcast(FP8X4),
+                    scales=scales[:, p, col0:col0 + GROUP],
+                    in_=grouped[g][:, p * 4 * GROUP:(p + 1) * 4 * GROUP],
                 )
 
-        for gi in range(6):
-            load(gi)
-
-        biases = {}
-
-        def bias_block(b):
+        def spread_bias(b):
             bias = keep.tile([P, D], F32, name="bias%d" % b, tag="bias%d" % b)
-            for c in range(2):
-                bb = psum.tile([P, 512], F32, name="bb", tag="bank")
-                lo = b * D + c * 512
-                nc.tensor.matmul(bb[:], lhsT=ones_b[:], rhs=brow[:, lo:lo + 512], start=True, stop=True)
-                nc.vector.tensor_copy(
-                    out=bias[:, c * 512:(c + 1) * 512].rearrange("p (j r) -> p j r", j=4),
-                    in_=bb[:].rearrange("p (r j) -> p j r", j=4),
-                )
             biases[b] = bias
+            for c in range(2):
+                bank = psum.tile([P, BANK], F32, name="bb", tag="bank")
+                lo = b * D + c * BANK
+                nc.tensor.matmul(bank[:], lhsT=ones_b[:], rhs=brow[:, lo:lo + BANK], start=True, stop=True)
+                nc.scalar.copy(
+                    out=bias[:, c * BANK:(c + 1) * BANK].rearrange("p (j r) -> p j r", j=4),
+                    in_=bank[:].rearrange("p (r j) -> p j r", j=4),
+                )
 
-        t_f = keep.tile([P, 1], F32, name="t_f", tag="t_f")
-        nc.vector.tensor_copy(out=t_f[:], in_=t_bf[:])
-        inv_t = keep.tile([P, 1], F32, name="inv_t", tag="inv_t")
-        nc.vector.reciprocal(out=inv_t[:], in_=t_f[:])
-
-        ys, rs, sss, g2s = {}, {}, {}, {}
-
-        def operands(i):
-            if i < 8:
-                return hm_c, hm_s, wm_c, wm_s, biases[0], i
-            return hp_c, hp_s, wp_c, wp_s, biases[1], i - 8
-
-        def a_block(k):
-            for e in range(2):
-                i = 2 * k + e
-                hc, hs, wc, ws, bias, rt = operands(i)
-                y = yp.tile([P, D], F32, name="y", tag="y")
+        def project(k):
+            for i in (2 * k, 2 * k + 1):
+                if i < MOL_TILES:
+                    hc, hs, wc, ws, bias, rows = hm_c, hm_s, wm_c, wm_s, biases[0], slice(i * P, (i + 1) * P)
+                else:
+                    hc, hs, wc, ws, bias = hp_c, hp_s, wp_c, wp_s, biases[1]
+                    rows = slice((i - MOL_TILES) * P, (i - MOL_TILES + 1) * P)
+                y = work.tile([P, D], F32, name="y", tag="y", bufs=6)
                 ys[i] = y
                 for c in range(2):
-                    x = psum.tile([P, 512], F32, name="x", tag="bank")
-                    for g in range(2):
+                    cols = slice(c * BANK, (c + 1) * BANK)
+                    bank = psum.tile([P, BANK], F32, name="x", tag="bank")
+                    for p in range(2):
                         nc.tensor.matmul_mx(
-                            out=x[:],
-                            lhsT=hc[:, g, rt * P:(rt + 1) * P].bitcast(FP8X4),
-                            lhsT_scale=hs[:, g, rt * P:(rt + 1) * P],
-                            rhs=wc[:, g, c * 512:(c + 1) * 512].bitcast(FP8X4),
-                            rhs_scale=ws[:, g, c * 512:(c + 1) * 512],
-                            start=(g == 0),
-                            stop=(g == 1),
+                            out=bank[:],
+                            lhsT=hc[:, p, rows].bitcast(FP8X4),
+                            lhsT_scale=hs[:, p, rows],
+                            rhs=wc[:, p, cols].bitcast(FP8X4),
+                            rhs_scale=ws[:, p, cols],
+                            start=(p == 0),
+                            stop=(p == 1),
                         )
-                    nc.vector.tensor_tensor(
-                        out=y[:, c * 512:(c + 1) * 512], in0=x[:], in1=bias[:, c * 512:(c + 1) * 512], op=ALU.add
-                    )
+                    nc.vector.tensor_tensor(out=y[:, cols], in0=bank[:], in1=bias[:, cols], op=ALU.add)
 
-        def w_block(k):
-            ss = wrk.tile([P, 2], F32, name="ss", tag="ss", bufs=4)
+        def row_norms(k):
+            ss = work.tile([P, 2], F32, name="ss", tag="ss", bufs=4)
             for e in range(2):
-                junk = wrk.tile([P, D], BF16, name="junk", tag="junk", bufs=1)
-                nc.scalar.activation(out=junk[:], in_=ys[2 * k + e][:], func=ACT.Square, accum_out=ss[:, e:e + 1])
-            nrm = wrk.tile([P, 2], F32, name="nrm", tag="nrm", bufs=4)
-            nc.scalar.sqrt(nrm[:], ss[:])
-            sss[k] = nrm
+                squares = work.tile([P, D], BF16, name="squares", tag="squares", bufs=1)
+                nc.scalar.activation(out=squares[:], in_=ys[2 * k + e][:], func=ACT.Square, accum_out=ss[:, e:e + 1])
+            norm = work.tile([P, 2], F32, name="norm", tag="norm", bufs=4)
+            nc.scalar.sqrt(norm[:], ss[:])
+            norms[k] = norm
 
-        def n_block(k):
-            nrm = sss[k]
-            r = wrk.tile([P, 2], F32, name="r", tag="r", bufs=4)
-            nc.vector.tensor_scalar_max(out=r[:], in0=nrm[:], scalar1=EPS)
+        def normalise(k):
+            r = work.tile([P, 2], F32, name="r", tag="r", bufs=4)
+            nc.vector.tensor_scalar_max(out=r[:], in0=norms[k][:], scalar1=EPS)
             nc.vector.reciprocal(out=r[:], in_=r[:])
             for e in range(2):
-                i = 2 * k + e
-                z = wrk.tile([P, D], BF16, name="z", tag="z", bufs=6)
+                z = work.tile([P, D], BF16, name="z", tag="z", bufs=6)
+                zs[2 * k + e] = z
                 nc.gpsimd.tensor_scalar(
-                    out=z[:], in0=ys[i][:], scalar1=r[:, e:e + 1], scalar2=0.0, op0=ALU.mult, op1=ALU.add
+                    out=z[:], in0=ys[2 * k + e][:], scalar1=r[:, e:e + 1], scalar2=0.0, op0=ALU.mult, op1=ALU.add
                 )
-                rs[i] = z
 
-        def b_block(k):
-            for e in range(2):
-                i = 2 * k + e
-                z = rs[i]
-                t2 = psum.tile([P, 8, P], BF16, name="t2", tag="bank")
+        def transpose_rows(k):
+            for i in (2 * k, 2 * k + 1):
+                bank = psum.tile([P, 8, P], BF16, name="t2", tag="bank")
                 for tau in range(8):
-                    nc.tensor.transpose(t2[:, tau, :], z[:, tau * P:(tau + 1) * P], ident_b[:])
-                g2 = wrk.tile([P, D], BF16, name="g2", tag="g2", bufs=4, align_bytes=64)
-                g2s[i] = g2
+                    nc.tensor.transpose(bank[:, tau, :], zs[i][:, tau * P:(tau + 1) * P], ident_b[:])
+                g2 = work.tile([P, D], BF16, name="g2", tag="g2", bufs=4, align_bytes=64)
+                regrouped[i] = g2
                 dst = g2[:].rearrange("p (c m j) -> p c m j", c=2, m=P, j=4)
-                src = t2[:].rearrange("p (c j) m -> p c m j", c=2, j=4)
-                if i % 2 == 1 and i < 8:
+                src = bank[:].rearrange("p (c j) m -> p c m j", c=2, j=4)
+                if i % 2 == 1 and 1 <= k < 6:
                     nc.scalar.copy(out=dst, in_=src)
                 else:
                     nc.vector.tensor_copy(out=dst, in_=src)
 
-        def r_block(i):
-            g2 = g2s[i]
-            if i < 8:
-                for c in range(2):
-                    nc.vector.quantize_mx(
-                        out=mn_c[:, c, i * P:(i + 1) * P].bitcast(FP8X4),
-                        scales=mn_s[:, c, i * P:(i + 1) * P],
-                        in_=g2[:, c * 512:(c + 1) * 512],
-                    )
-            else:
-                nc.vector.quantize_mx(out=pn_c[:, i - 8, :].bitcast(FP8X4), scales=pn_s[:, i - 8, :], in_=g2[:])
+        def quantise_rows(k):
+            for i in (2 * k, 2 * k + 1):
+                g2 = regrouped[i]
+                if i < MOL_TILES:
+                    for c in range(2):
+                        nc.vector.quantize_mx(
+                            out=mn_c[:, c, i * P:(i + 1) * P].bitcast(FP8X4),
+                            scales=mn_s[:, c, i * P:(i + 1) * P],
+                            in_=g2[:, c * BANK:(c + 1) * BANK],
+                        )
+                else:
+                    rt = i - MOL_TILES
+                    nc.vector.quantize_mx(out=pn_c[:, rt, :].bitcast(FP8X4), scales=pn_s[:, rt, :], in_=g2[:])
 
-        def c_block(k):
-            for e in range(2):
-                rt = 2 * k + e - 8
-                osb = wrk.tile([P, N_MOL], F32, name="osb", tag="osb", bufs=4)
+        def similarity(k):
+            for rt in (2 * k - MOL_TILES, 2 * k + 1 - MOL_TILES):
+                osb = work.tile([P, N_MOL], F32, name="osb", tag="osb", bufs=4)
                 for nh in range(2):
-                    o = psum.tile([P, 512], F32, name="o", tag="bank")
+                    cols = slice(nh * BANK, (nh + 1) * BANK)
+                    bank = psum.tile([P, BANK], F32, name="o", tag="bank")
                     for c in range(2):
                         nc.tensor.matmul_mx(
-                            out=o[:],
+                            out=bank[:],
                             lhsT=pn_c[:, rt, c * P:(c + 1) * P].bitcast(FP8X4),
                             lhsT_scale=pn_s[:, rt, c * P:(c + 1) * P],
-                            rhs=mn_c[:, c, nh * 512:(nh + 1) * 512].bitcast(FP8X4),
-                            rhs_scale=mn_s[:, c, nh * 512:(nh + 1) * 512],
+                            rhs=mn_c[:, c, cols].bitcast(FP8X4),
+                            rhs_scale=mn_s[:, c, cols],
                             start=(c == 0),
                             stop=(c == 1),
                         )
-                    if rt >= 12 and nh == 1:
-                        nc.vector.tensor_scalar_mul(out=osb[:, nh * 512:(nh + 1) * 512], in0=o[:], scalar1=inv_t[:, 0:1])
+                    if rt >= 13 and nh == 1:
+                        nc.vector.tensor_scalar_mul(out=osb[:, cols], in0=bank[:], scalar1=inv_t[:, 0:1])
                     else:
-                        nc.scalar.activation(
-                            out=osb[:, nh * 512:(nh + 1) * 512], in_=o[:], func=ACT.Copy, scale=inv_t[:, 0:1]
-                        )
+                        nc.scalar.activation(out=osb[:, cols], in_=bank[:], func=ACT.Copy, scale=inv_t[:, 0:1])
                 nc.sync.dma_start(out=out[rt * P:(rt + 1) * P, :], in_=osb[:])
 
-        seq = [
-            ("S", 1), ("S", 0), ("I", 0), ("Q", 0), ("I", 1), ("Q", 1), ("I", 2), ("I", 3), ("Q", 2), ("A", 0),
-            ("W", 0), ("Q", 3), ("I", 4), ("A", 1), ("W", 1), ("N", 0), ("A", 2), ("Q", 4), ("N", 1), ("I", 6),
-            ("I", 5), ("A", 3), ("W", 2), ("B", 0), ("Q", 6), ("Q", 5), ("I", 7), ("N", 2), ("A", 4), ("W", 3),
-            ("B", 1), ("r", 0), ("r", 2), ("Q", 7), ("r", 1), ("A", 5), ("N", 3), ("W", 4), ("r", 3), ("B", 2),
-            ("r", 4), ("N", 4), ("A", 6), ("I", 8), ("r", 5), ("W", 5), ("B", 3), ("B", 4), ("r", 8), ("Q", 8),
-            ("W", 6), ("I", 9), ("r", 7), ("N", 5), ("r", 9), ("A", 7), ("r", 6), ("N", 6), ("A", 8), ("C", 4),
-            ("Q", 9), ("B", 5), ("r", 10), ("W", 7), ("W", 8), ("r", 11), ("N", 7), ("B", 6), ("A", 9), ("C", 5),
-            ("r", 13), ("r", 12), ("N", 8), ("B", 7), ("W", 9), ("r", 14), ("A", 10), ("C", 6), ("r", 15), ("N", 9),
-            ("W", 10), ("B", 8), ("r", 17), ("C", 7), ("r", 16), ("N", 10), ("A", 11), ("W", 11), ("B", 9), ("C", 8),
-            ("r", 18), ("r", 19), ("N", 11), ("B", 10), ("r", 20), ("r", 21), ("C", 9), ("B", 11), ("r", 22), ("C", 10),
-            ("r", 23), ("C", 11),
-        ]
-        kinds = {
-            "I": in_block, "Q": q_block, "S": bias_block, "A": a_block, "W": w_block, "N": n_block,
-            "B": b_block, "r": r_block, "C": c_block,
-        }
-        for step in seq:
-            kinds[step[0]](step[1])
+        transpose_group(0)
+        quantise_group(0)
+        spread_bias(0)
+        transpose_group(1)
+        quantise_group(1)
+        temperature_reciprocal()
+        transpose_group(2)
+        quantise_group(2)
+        spread_bias(1)
+        transpose_group(3)
+        for k in range(PAIRS + 4):
+            if k < PAIRS:
+                project(k)
+            if k + 3 < len(groups):
+                quantise_group(k + 3)
+            if 0 <= k - 1 < PAIRS:
+                normalise(k - 1)
+            if 0 <= k - 3 < PAIRS:
+                quantise_rows(k - 3)
+            if MOL_PAIRS <= k - 4 < PAIRS:
+                similarity(k - 4)
+            if k + 4 < len(groups):
+                transpose_group(k + 4)
+            if 0 <= k - 2 < PAIRS:
+                transpose_rows(k - 2)
+            if k < PAIRS:
+                row_norms(k)

@@ -45,19 +45,16 @@ def tile_coembedding_pa_kernel(tc, h_mol, h_prot, Wm2, bm2, Wp2, bp2, temperatur
         mn_c, mn_s = codes_and_scales("mn", [P, 2, N_MOL])
         pn_c, pn_s = codes_and_scales("pn", [P, N_PROT // P, 2 * P])
 
-        def w_rows(w, c):
-            return w.rearrange("(c r j) f -> c r j f", c=2, r=P, j=4)[c]
-
         def h_rows(h, g):
             return h[g * GROUP:(g + 1) * GROUP, :].rearrange("(t r) f -> r t f", t=4)
 
         groups = [
-            (w_rows(Wm2, 0), wm_c, wm_s, 0),
-            (w_rows(Wm2, 1), wm_c, wm_s, GROUP),
+            (h_rows(Wm2, 0), wm_c, wm_s, 0),
+            (h_rows(Wm2, 1), wm_c, wm_s, GROUP),
             (h_rows(h_mol, 0), hm_c, hm_s, 0),
             (h_rows(h_mol, 1), hm_c, hm_s, GROUP),
-            (w_rows(Wp2, 0), wp_c, wp_s, 0),
-            (w_rows(Wp2, 1), wp_c, wp_s, GROUP),
+            (h_rows(Wp2, 0), wp_c, wp_s, 0),
+            (h_rows(Wp2, 1), wp_c, wp_s, GROUP),
             (h_rows(h_prot, 0), hp_c, hp_s, 0),
             (h_rows(h_prot, 1), hp_c, hp_s, GROUP),
             (h_rows(h_prot, 2), hp_c, hp_s, 2 * GROUP),
@@ -83,8 +80,6 @@ def tile_coembedding_pa_kernel(tc, h_mol, h_prot, Wm2, bm2, Wp2, bp2, temperatur
         nc.scalar.sqrt(warm[:], warm[:])
         ident_f = keep.tile([P, P], F32, name="ident_f", tag="ident_f")
         masks.make_identity(nc, ident_f[:])
-        ident_b = keep.tile([P, P], BF16, name="ident_b", tag="ident_b")
-        masks.make_identity(nc, ident_b[:])
         ones_b = keep.tile([P, P], BF16, name="ones_b", tag="ones_b")
         nc.vector.memset(ones_b[:], 1.0)
         t_f = keep.tile([P, 1], F32, name="t_f", tag="t_f")
@@ -129,10 +124,7 @@ def tile_coembedding_pa_kernel(tc, h_mol, h_prot, Wm2, bm2, Wp2, bp2, temperatur
                 bank = psum.tile([P, BANK], F32, name="bb", tag="bank")
                 lo = b * D + c * BANK
                 nc.tensor.matmul(bank[:], lhsT=ones_b[:], rhs=brow[:, lo:lo + BANK], start=True, stop=True)
-                nc.scalar.copy(
-                    out=bias[:, c * BANK:(c + 1) * BANK].rearrange("p (j r) -> p j r", j=4),
-                    in_=bank[:].rearrange("p (r j) -> p j r", j=4),
-                )
+                nc.scalar.copy(out=bias[:, c * BANK:(c + 1) * BANK], in_=bank[:])
 
         def project(k):
             for i in (2 * k, 2 * k + 1):
@@ -180,13 +172,14 @@ def tile_coembedding_pa_kernel(tc, h_mol, h_prot, Wm2, bm2, Wp2, bp2, temperatur
 
         def transpose_rows(k):
             for i in (2 * k, 2 * k + 1):
-                bank = psum.tile([P, 8, P], BF16, name="t2", tag="bank")
-                for tau in range(8):
-                    nc.tensor.transpose(bank[:, tau, :], zs[i][:, tau * P:(tau + 1) * P], ident_b[:])
+                words = zs[i][:].bitcast(F32)
+                bank = psum.tile([P, 4, P], F32, name="t2", tag="bank")
+                for cu in range(4):
+                    nc.tensor.transpose(bank[:, cu, :], words[:, cu * P:(cu + 1) * P], ident_f[:])
                 g2 = work.tile([P, D], BF16, name="g2", tag="g2", bufs=4, align_bytes=64)
                 regrouped[i] = g2
-                dst = g2[:].rearrange("p (c m j) -> p c m j", c=2, m=P, j=4)
-                src = bank[:].rearrange("p (c j) m -> p c m j", c=2, j=4)
+                dst = g2[:].bitcast(F32).rearrange("p (c m u) -> p c m u", c=2, m=P, u=2)
+                src = bank[:].rearrange("p (c u) m -> p c m u", c=2, u=2)
                 if i % 2 == 1 and 1 <= k < 6:
                     nc.scalar.copy(out=dst, in_=src)
                 else:

@@ -17,12 +17,13 @@ EPS = 1e-8
 FLOPS = 2 * (N_MOL * F * D + N_PROT * F * D + N_PROT * N_MOL * D)
 
 BANK = 512
-GROUP = 4 * P
+GROUP = 2 * P
 MOL_TILES = N_MOL // P
 TILES = (N_MOL + N_PROT) // P
 PAIRS = TILES // 2
 MOL_PAIRS = MOL_TILES // 2
-RAW_BUFS = 6
+RAW_BUFS = 24
+WARMUPS = 8
 
 
 def tile_coembedding_pa_kernel(tc, h_mol, h_prot, Wm2, bm2, Wp2, bp2, temperature, out):
@@ -45,43 +46,46 @@ def tile_coembedding_pa_kernel(tc, h_mol, h_prot, Wm2, bm2, Wp2, bp2, temperatur
         mn_c, mn_s = codes_and_scales("mn", [P, 2, N_MOL])
         pn_c, pn_s = codes_and_scales("pn", [P, N_PROT // P, 2 * P])
 
-        def h_rows(h, g):
-            return h[g * GROUP:(g + 1) * GROUP, :].rearrange("(t r) f -> r t f", t=4)
+        groups = {}
+        for label, src, codes, scales, n in (
+            ("wm", Wm2, wm_c, wm_s, 4), ("hm", h_mol, hm_c, hm_s, 4), ("wp", Wp2, wp_c, wp_s, 4), ("hp", h_prot, hp_c, hp_s, 8),
+        ):
+            for j in range(n):
+                groups[label, j] = (src, j * GROUP, codes, scales)
+        load_order = [("wm", 0), ("wm", 1), ("hm", 0), ("hm", 1), ("wm", 2), ("wm", 3), ("hm", 2), ("hm", 3)]
+        load_order += [("wp", j) for j in range(4)]
+        load_order += [("hp", j) for j in range(8)]
+        load_order = [(g, t) for g in load_order for t in range(2)]
+        raws, grouped, biases, ys, norms, rs, zs, regrouped = {}, {}, {}, {}, {}, {}, {}, {}
 
-        groups = [
-            (h_rows(Wm2, 0), wm_c, wm_s, 0),
-            (h_rows(Wm2, 1), wm_c, wm_s, GROUP),
-            (h_rows(h_mol, 0), hm_c, hm_s, 0),
-            (h_rows(h_mol, 1), hm_c, hm_s, GROUP),
-            (h_rows(Wp2, 0), wp_c, wp_s, 0),
-            (h_rows(Wp2, 1), wp_c, wp_s, GROUP),
-            (h_rows(h_prot, 0), hp_c, hp_s, 0),
-            (h_rows(h_prot, 1), hp_c, hp_s, GROUP),
-            (h_rows(h_prot, 2), hp_c, hp_s, 2 * GROUP),
-            (h_rows(h_prot, 3), hp_c, hp_s, 3 * GROUP),
-        ]
-        raws, grouped, biases, ys, norms, zs, regrouped = {}, {}, {}, {}, {}, {}, {}
-
-        def load(g):
-            raws[g] = work.tile([P, 4, F], BF16, name="raw", tag="raw", bufs=RAW_BUFS)
-            nc.sync.dma_start(out=raws[g][:], in_=groups[g][0])
+        def load(n):
+            if n < len(load_order):
+                g, t = load_order[n]
+                src, row0 = groups[g][0], groups[g][1] + t * P
+                raw = work.tile([P, F], BF16, name="raw", tag="raw", bufs=RAW_BUFS)
+                raws[g, t] = raw
+                nc.sync.dma_start(out=raw[:], in_=src[row0:row0 + P, :])
 
         brow = keep.tile([P, 2 * D], BF16, name="brow", tag="brow")
+        ones_b = keep.tile([P, P], BF16, name="ones_b", tag="ones_b")
+        nc.vector.memset(ones_b[:], 1.0)
+        zeros_b = keep.tile([P, BANK], BF16, name="zeros_b", tag="zeros_b")
+        nc.vector.memset(zeros_b[:], 0.0)
         nc.vector.memset(brow[:], 0.0)
         t_bf = keep.tile([P, 1], BF16, name="t_bf", tag="t_bf")
         nc.scalar.dma_start(out=t_bf[:], in_=temperature.partition_broadcast(P))
-        load(0)
+        for n in range(8):
+            load(n)
         nc.sync.dma_start(out=brow[0:1, 0:D], in_=bm2.rearrange("(o n) -> o n", o=1))
         nc.sync.dma_start(out=brow[0:1, D:2 * D], in_=bp2.rearrange("(o n) -> o n", o=1))
-        for g in range(1, RAW_BUFS):
-            load(g)
+        for n in range(8, RAW_BUFS):
+            load(n)
+        next_load = [RAW_BUFS]
         warm = keep.tile([P, 1], F32, name="warm", tag="warm")
         nc.vector.memset(warm[:], 1.0)
         nc.scalar.sqrt(warm[:], warm[:])
         ident_f = keep.tile([P, P], F32, name="ident_f", tag="ident_f")
         masks.make_identity(nc, ident_f[:])
-        ones_b = keep.tile([P, P], BF16, name="ones_b", tag="ones_b")
-        nc.vector.memset(ones_b[:], 1.0)
         t_f = keep.tile([P, 1], F32, name="t_f", tag="t_f")
         inv_t = keep.tile([P, 1], F32, name="inv_t", tag="inv_t")
 
@@ -89,33 +93,38 @@ def tile_coembedding_pa_kernel(tc, h_mol, h_prot, Wm2, bm2, Wp2, bp2, temperatur
             nc.vector.tensor_copy(out=t_f[:], in_=t_bf[:])
             nc.vector.reciprocal(out=inv_t[:], in_=t_f[:])
 
-        def transpose_group(g):
-            words = raws[g][:].rearrange("p t f -> p (t f)").bitcast(F32)
-            grp = work.tile([P, 4 * 2 * BANK], BF16, name="grp", tag="grp", bufs=3, align_bytes=64)
+        def copy_out(engine, out, in_):
+            if engine == "v":
+                nc.vector.tensor_copy(out=out, in_=in_)
+            else:
+                nc.scalar.copy(out=out, in_=in_)
+
+        def transpose_in(g, engines):
+            grp = work.tile([P, 8 * GROUP], BF16, name="grp", tag="grp", bufs=6, align_bytes=64)
             grouped[g] = grp
-            grp_words = grp[:].bitcast(F32).rearrange("q (g n u) -> q g n u", g=2, n=GROUP, u=2)
-            for t in range(4):
+            grp_words = grouped[g][:].bitcast(F32).rearrange("q (g n u) -> q g n u", g=2, n=GROUP, u=2)
+            for t, engine in enumerate(engines):
+                words = raws[g, t][:].bitcast(F32)
                 bank = psum.tile([P, 4, P], F32, name="tin", tag="bank")
                 for gu in range(4):
-                    lo = t * BANK + gu * P
-                    nc.tensor.transpose(bank[:, gu, :], words[:, lo:lo + P], ident_f[:])
-                src = bank[:].rearrange("q (g u) r -> q g r u", g=2, u=2)
-                dst = grp_words[:, :, t * P:(t + 1) * P, :]
-                if (g < 3 and t % 2 == 1) or (3 <= g < 6 and t == 3):
-                    nc.vector.tensor_copy(out=dst, in_=src)
-                else:
-                    nc.scalar.copy(out=dst, in_=src)
-            if g + RAW_BUFS < len(groups):
-                load(g + RAW_BUFS)
+                    nc.tensor.transpose(bank[:, gu, :], words[:, gu * P:(gu + 1) * P], ident_f[:])
+                copy_out(engine, grp_words[:, :, t * P:(t + 1) * P, :], bank[:].rearrange("q (g u) r -> q g r u", g=2, u=2))
+                load(next_load[0])
+                next_load[0] += 1
 
-        def quantise_group(g):
-            codes, scales, col0 = groups[g][1], groups[g][2], groups[g][3]
+        def quantise_in(g):
+            codes, scales, col0 = groups[g][2], groups[g][3], groups[g][1]
             for p in range(2):
                 nc.vector.quantize_mx(
                     out=codes[:, p, col0:col0 + GROUP].bitcast(FP8X4),
                     scales=scales[:, p, col0:col0 + GROUP],
                     in_=grouped[g][:, p * 4 * GROUP:(p + 1) * 4 * GROUP],
                 )
+
+        def warm_up(n):
+            bank = psum.tile([P, BANK], F32, name="wu", tag="bank")
+            for m in range(n):
+                nc.tensor.matmul(bank[:], lhsT=ones_b[:], rhs=zeros_b[:], start=True, stop=True)
 
         def spread_bias(b):
             bias = keep.tile([P, D], F32, name="bias%d" % b, tag="bias%d" % b)
@@ -126,29 +135,29 @@ def tile_coembedding_pa_kernel(tc, h_mol, h_prot, Wm2, bm2, Wp2, bp2, temperatur
                 nc.tensor.matmul(bank[:], lhsT=ones_b[:], rhs=brow[:, lo:lo + BANK], start=True, stop=True)
                 nc.scalar.copy(out=bias[:, c * BANK:(c + 1) * BANK], in_=bank[:])
 
-        def project(k):
-            for i in (2 * k, 2 * k + 1):
-                if i < MOL_TILES:
-                    hc, hs, wc, ws, bias, rows = hm_c, hm_s, wm_c, wm_s, biases[0], slice(i * P, (i + 1) * P)
-                else:
-                    hc, hs, wc, ws, bias = hp_c, hp_s, wp_c, wp_s, biases[1]
-                    rows = slice((i - MOL_TILES) * P, (i - MOL_TILES + 1) * P)
+        def project(i, halves=(0, 1)):
+            if i < MOL_TILES:
+                hc, hs, wc, ws, bias, rows = hm_c, hm_s, wm_c, wm_s, biases[0], slice(i * P, (i + 1) * P)
+            else:
+                hc, hs, wc, ws, bias = hp_c, hp_s, wp_c, wp_s, biases[1]
+                rows = slice((i - MOL_TILES) * P, (i - MOL_TILES + 1) * P)
+            if i not in ys:
                 y = work.tile([P, D], F32, name="y", tag="y", bufs=6)
                 ys[i] = y
-                for c in range(2):
-                    cols = slice(c * BANK, (c + 1) * BANK)
-                    bank = psum.tile([P, BANK], F32, name="x", tag="bank")
-                    for p in range(2):
-                        nc.tensor.matmul_mx(
-                            out=bank[:],
-                            lhsT=hc[:, p, rows].bitcast(FP8X4),
-                            lhsT_scale=hs[:, p, rows],
-                            rhs=wc[:, p, cols].bitcast(FP8X4),
-                            rhs_scale=ws[:, p, cols],
-                            start=(p == 0),
-                            stop=(p == 1),
-                        )
-                    nc.vector.tensor_tensor(out=y[:, cols], in0=bank[:], in1=bias[:, cols], op=ALU.add)
+            for c in halves:
+                cols = slice(c * BANK, (c + 1) * BANK)
+                bank = psum.tile([P, BANK], F32, name="x", tag="bank")
+                for p in range(2):
+                    nc.tensor.matmul_mx(
+                        out=bank[:],
+                        lhsT=hc[:, p, rows].bitcast(FP8X4),
+                        lhsT_scale=hs[:, p, rows],
+                        rhs=wc[:, p, cols].bitcast(FP8X4),
+                        rhs_scale=ws[:, p, cols],
+                        start=(p == 0),
+                        stop=(p == 1),
+                    )
+                nc.vector.tensor_tensor(out=ys[i][:, cols], in0=bank[:], in1=bias[:, cols], op=ALU.add)
 
         def row_norms(k):
             ss = work.tile([P, 2], F32, name="ss", tag="ss", bufs=4)
@@ -159,92 +168,104 @@ def tile_coembedding_pa_kernel(tc, h_mol, h_prot, Wm2, bm2, Wp2, bp2, temperatur
             nc.scalar.sqrt(norm[:], ss[:])
             norms[k] = norm
 
-        def normalise(k):
+        def clamp(k):
             r = work.tile([P, 2], F32, name="r", tag="r", bufs=4)
+            rs[k] = r
             nc.vector.tensor_scalar_max(out=r[:], in0=norms[k][:], scalar1=EPS)
-            nc.vector.reciprocal(out=r[:], in_=r[:])
+
+        def normalise(k):
+            nc.vector.reciprocal(out=rs[k][:], in_=rs[k][:])
             for e in range(2):
                 z = work.tile([P, D], BF16, name="z", tag="z", bufs=6)
                 zs[2 * k + e] = z
                 nc.gpsimd.tensor_scalar(
-                    out=z[:], in0=ys[2 * k + e][:], scalar1=r[:, e:e + 1], scalar2=0.0, op0=ALU.mult, op1=ALU.add
+                    out=z[:], in0=ys[2 * k + e][:], scalar1=rs[k][:, e:e + 1], scalar2=0.0, op0=ALU.mult, op1=ALU.add
                 )
 
-        def transpose_rows(k):
-            for i in (2 * k, 2 * k + 1):
-                words = zs[i][:].bitcast(F32)
-                bank = psum.tile([P, 4, P], F32, name="t2", tag="bank")
-                for cu in range(4):
-                    nc.tensor.transpose(bank[:, cu, :], words[:, cu * P:(cu + 1) * P], ident_f[:])
-                g2 = work.tile([P, D], BF16, name="g2", tag="g2", bufs=4, align_bytes=64)
-                regrouped[i] = g2
-                dst = g2[:].bitcast(F32).rearrange("p (c m u) -> p c m u", c=2, m=P, u=2)
-                src = bank[:].rearrange("p (c u) m -> p c m u", c=2, u=2)
-                if i % 2 == 1 and 1 <= k < 6:
-                    nc.scalar.copy(out=dst, in_=src)
+        def transpose_rows(i, engine):
+            words = zs[i][:].bitcast(F32)
+            bank = psum.tile([P, 4, P], F32, name="t2", tag="bank")
+            for cu in range(4):
+                nc.tensor.transpose(bank[:, cu, :], words[:, cu * P:(cu + 1) * P], ident_f[:])
+            g2 = work.tile([P, D], BF16, name="g2", tag="g2", bufs=4, align_bytes=64)
+            regrouped[i] = g2
+            dst = g2[:].bitcast(F32).rearrange("p (c m u) -> p c m u", c=2, m=P, u=2)
+            copy_out(engine, dst, bank[:].rearrange("p (c u) m -> p c m u", c=2, u=2))
+
+        def quantise_rows(i):
+            g2 = regrouped[i]
+            if i < MOL_TILES:
+                for c in range(2):
+                    nc.vector.quantize_mx(
+                        out=mn_c[:, c, i * P:(i + 1) * P].bitcast(FP8X4),
+                        scales=mn_s[:, c, i * P:(i + 1) * P],
+                        in_=g2[:, c * BANK:(c + 1) * BANK],
+                    )
+            else:
+                rt = i - MOL_TILES
+                nc.vector.quantize_mx(out=pn_c[:, rt, :].bitcast(FP8X4), scales=pn_s[:, rt, :], in_=g2[:])
+
+        def similarity(i, engines):
+            rt = i - MOL_TILES
+            osb = work.tile([P, N_MOL], F32, name="osb", tag="osb", bufs=5)
+            for nh in range(2):
+                cols = slice(nh * BANK, (nh + 1) * BANK)
+                bank = psum.tile([P, BANK], F32, name="o", tag="bank")
+                for c in range(2):
+                    nc.tensor.matmul_mx(
+                        out=bank[:],
+                        lhsT=pn_c[:, rt, c * P:(c + 1) * P].bitcast(FP8X4),
+                        lhsT_scale=pn_s[:, rt, c * P:(c + 1) * P],
+                        rhs=mn_c[:, c, cols].bitcast(FP8X4),
+                        rhs_scale=mn_s[:, c, cols],
+                        start=(c == 0),
+                        stop=(c == 1),
+                    )
+                if engines[nh] == "v":
+                    nc.vector.tensor_scalar_mul(out=osb[:, cols], in0=bank[:], scalar1=inv_t[:, 0:1])
                 else:
-                    nc.vector.tensor_copy(out=dst, in_=src)
+                    nc.scalar.activation(out=osb[:, cols], in_=bank[:], func=ACT.Copy, scale=inv_t[:, 0:1])
+            nc.sync.dma_start(out=out[rt * P:(rt + 1) * P, :], in_=osb[:])
 
-        def quantise_rows(k):
-            for i in (2 * k, 2 * k + 1):
-                g2 = regrouped[i]
-                if i < MOL_TILES:
-                    for c in range(2):
-                        nc.vector.quantize_mx(
-                            out=mn_c[:, c, i * P:(i + 1) * P].bitcast(FP8X4),
-                            scales=mn_s[:, c, i * P:(i + 1) * P],
-                            in_=g2[:, c * BANK:(c + 1) * BANK],
-                        )
-                else:
-                    rt = i - MOL_TILES
-                    nc.vector.quantize_mx(out=pn_c[:, rt, :].bitcast(FP8X4), scales=pn_s[:, rt, :], in_=g2[:])
-
-        def similarity(k):
-            for rt in (2 * k - MOL_TILES, 2 * k + 1 - MOL_TILES):
-                osb = work.tile([P, N_MOL], F32, name="osb", tag="osb", bufs=4)
-                for nh in range(2):
-                    cols = slice(nh * BANK, (nh + 1) * BANK)
-                    bank = psum.tile([P, BANK], F32, name="o", tag="bank")
-                    for c in range(2):
-                        nc.tensor.matmul_mx(
-                            out=bank[:],
-                            lhsT=pn_c[:, rt, c * P:(c + 1) * P].bitcast(FP8X4),
-                            lhsT_scale=pn_s[:, rt, c * P:(c + 1) * P],
-                            rhs=mn_c[:, c, cols].bitcast(FP8X4),
-                            rhs_scale=mn_s[:, c, cols],
-                            start=(c == 0),
-                            stop=(c == 1),
-                        )
-                    if rt >= 13 and nh == 1:
-                        nc.vector.tensor_scalar_mul(out=osb[:, cols], in0=bank[:], scalar1=inv_t[:, 0:1])
-                    else:
-                        nc.scalar.activation(out=osb[:, cols], in_=bank[:], func=ACT.Copy, scale=inv_t[:, 0:1])
-                nc.sync.dma_start(out=out[rt * P:(rt + 1) * P, :], in_=osb[:])
-
-        transpose_group(0)
-        quantise_group(0)
+        tin = {0: (("hm", 2), ("hm", 3), ("wp", 0)), 1: (("wp", 1), ("wp", 2)), 2: (("wp", 3), ("hp", 0)), 3: (("hp", 1),),
+               4: (("hp", 2), ("hp", 3)), 5: (("hp", 4),), 6: (("hp", 5), ("hp", 6)), 7: (("hp", 7),)}
+        warm_up(WARMUPS)
+        transpose_in(("wm", 0), "vs")
+        transpose_in(("wm", 1), "vs")
+        quantise_in(("wm", 0))
+        transpose_in(("hm", 0), "vs")
+        quantise_in(("wm", 1))
+        transpose_in(("hm", 1), "vs")
+        quantise_in(("hm", 0))
+        quantise_in(("hm", 1))
         spread_bias(0)
-        transpose_group(1)
-        quantise_group(1)
+        transpose_in(("wm", 2), "vs")
+        transpose_in(("wm", 3), "vs")
         temperature_reciprocal()
-        transpose_group(2)
-        quantise_group(2)
-        spread_bias(1)
-        transpose_group(3)
+        quantise_in(("wm", 2))
+        quantise_in(("wm", 3))
         for k in range(PAIRS + 4):
             if k < PAIRS:
-                project(k)
-            if k + 3 < len(groups):
-                quantise_group(k + 3)
+                project(2 * k)
+                project(2 * k + 1)
+            for g in tin.get(k - 1, ()):
+                quantise_in(g)
+            if 0 <= k - 1 < PAIRS:
+                clamp(k - 1)
+            if 0 <= k - 3 < PAIRS:
+                quantise_rows(2 * (k - 3))
+                quantise_rows(2 * (k - 3) + 1)
             if 0 <= k - 1 < PAIRS:
                 normalise(k - 1)
-            if 0 <= k - 3 < PAIRS:
-                quantise_rows(k - 3)
             if MOL_PAIRS <= k - 4 < PAIRS:
-                similarity(k - 4)
-            if k + 4 < len(groups):
-                transpose_group(k + 4)
+                for i in (2 * (k - 4), 2 * (k - 4) + 1):
+                    similarity(i, "sv" if i % 3 == 1 else "ss")
+            for g in tin.get(k, ()):
+                transpose_in(g, "sv" if g[1] % 2 == 1 else "ss")
             if 0 <= k - 2 < PAIRS:
-                transpose_rows(k - 2)
+                for i in (2 * (k - 2), 2 * (k - 2) + 1):
+                    transpose_rows(i, "v" if i >= 12 or i % 4 == 3 else "s")
             if k < PAIRS:
                 row_norms(k)
+            if k == 0:
+                spread_bias(1)

@@ -44,7 +44,7 @@ def tile_coembedding_pa_kernel(tc, h_mol, h_prot, Wm2, bm2, Wp2, bp2, temperatur
         hm_c, hm_s = codes_and_scales("hm", [P, 2, N_MOL])
         hp_c, hp_s = codes_and_scales("hp", [P, 2, N_PROT])
         mn_c, mn_s = codes_and_scales("mn", [P, 2, N_MOL])
-        pn_c, pn_s = codes_and_scales("pn", [P, N_PROT // P, 2 * P])
+        pn_c, pn_s = codes_and_scales("pn", [P, N_PROT // GROUP, 2, GROUP])
 
         groups = {}
         for label, src, codes, scales, n in (
@@ -56,7 +56,7 @@ def tile_coembedding_pa_kernel(tc, h_mol, h_prot, Wm2, bm2, Wp2, bp2, temperatur
         load_order += [("wp", j) for j in range(4)]
         load_order += [("hp", j) for j in range(8)]
         load_order = [(g, t) for g in load_order for t in range(2)]
-        raws, grouped, biases, ys, norms, rs, zs, regrouped = {}, {}, {}, {}, {}, {}, {}, {}
+        raws, grouped, biases, ys, rs, zs, regrouped = {}, {}, {}, {}, {}, {}, {}
 
         def load(n):
             if n < len(load_order):
@@ -83,7 +83,7 @@ def tile_coembedding_pa_kernel(tc, h_mol, h_prot, Wm2, bm2, Wp2, bp2, temperatur
         next_load = [RAW_BUFS]
         warm = keep.tile([P, 1], F32, name="warm", tag="warm")
         nc.vector.memset(warm[:], 1.0)
-        nc.scalar.sqrt(warm[:], warm[:])
+        nc.scalar.activation(out=warm[:], in_=warm[:], func=ACT.Abs_reciprocal_sqrt)
         ident_f = keep.tile([P, P], F32, name="ident_f", tag="ident_f")
         masks.make_identity(nc, ident_f[:])
         t_f = keep.tile([P, 1], F32, name="t_f", tag="t_f")
@@ -164,22 +164,18 @@ def tile_coembedding_pa_kernel(tc, h_mol, h_prot, Wm2, bm2, Wp2, bp2, temperatur
             for e in range(2):
                 squares = work.tile([P, D], BF16, name="squares", tag="squares", bufs=1)
                 nc.scalar.activation(out=squares[:], in_=ys[2 * k + e][:], func=ACT.Square, accum_out=ss[:, e:e + 1])
-            norm = work.tile([P, 2], F32, name="norm", tag="norm", bufs=4)
-            nc.scalar.sqrt(norm[:], ss[:])
-            norms[k] = norm
-
-        def clamp(k):
             r = work.tile([P, 2], F32, name="r", tag="r", bufs=4)
+            nc.scalar.activation(out=r[:], in_=ss[:], func=ACT.Abs_reciprocal_sqrt)
             rs[k] = r
-            nc.vector.tensor_scalar_max(out=r[:], in0=norms[k][:], scalar1=EPS)
 
         def normalise(k):
-            nc.vector.reciprocal(out=rs[k][:], in_=rs[k][:])
+            rc = work.tile([P, 2], F32, name="rc", tag="rc", bufs=4)
+            nc.gpsimd.tensor_scalar(out=rc[:], in0=rs[k][:], scalar1=1.0 / EPS, scalar2=0.0, op0=ALU.min, op1=ALU.add)
             for e in range(2):
                 z = work.tile([P, D], BF16, name="z", tag="z", bufs=6)
                 zs[2 * k + e] = z
                 nc.gpsimd.tensor_scalar(
-                    out=z[:], in0=ys[2 * k + e][:], scalar1=rs[k][:, e:e + 1], scalar2=0.0, op0=ALU.mult, op1=ALU.add
+                    out=z[:], in0=ys[2 * k + e][:], scalar1=rc[:, e:e + 1], scalar2=0.0, op0=ALU.mult, op1=ALU.add
                 )
 
         def transpose_rows(i, engine):
@@ -187,26 +183,33 @@ def tile_coembedding_pa_kernel(tc, h_mol, h_prot, Wm2, bm2, Wp2, bp2, temperatur
             bank = psum.tile([P, 4, P], F32, name="t2", tag="bank")
             for cu in range(4):
                 nc.tensor.transpose(bank[:, cu, :], words[:, cu * P:(cu + 1) * P], ident_f[:])
-            g2 = work.tile([P, D], BF16, name="g2", tag="g2", bufs=4, align_bytes=64)
-            regrouped[i] = g2
-            dst = g2[:].bitcast(F32).rearrange("p (c m u) -> p c m u", c=2, m=P, u=2)
-            copy_out(engine, dst, bank[:].rearrange("p (c u) m -> p c m u", c=2, u=2))
+            if i % 2 == 0:
+                g2 = work.tile([P, 2 * D], BF16, name="g2", tag="g2", bufs=3, align_bytes=64)
+                regrouped[i // 2] = g2
+            dst = regrouped[i // 2][:].bitcast(F32).rearrange("p (c m u) -> p c m u", c=2, m=2 * P, u=2)
+            lo = (i % 2) * P
+            copy_out(engine, dst[:, :, lo:lo + P, :], bank[:].rearrange("p (c u) m -> p c m u", c=2, u=2))
 
-        def quantise_rows(i):
-            g2 = regrouped[i]
-            if i < MOL_TILES:
+        def quantise_rows(k):
+            g2 = regrouped[k]
+            if k < MOL_PAIRS:
                 for c in range(2):
                     nc.vector.quantize_mx(
-                        out=mn_c[:, c, i * P:(i + 1) * P].bitcast(FP8X4),
-                        scales=mn_s[:, c, i * P:(i + 1) * P],
-                        in_=g2[:, c * BANK:(c + 1) * BANK],
+                        out=mn_c[:, c, 2 * k * P:2 * (k + 1) * P].bitcast(FP8X4),
+                        scales=mn_s[:, c, 2 * k * P:2 * (k + 1) * P],
+                        in_=g2[:, c * D:(c + 1) * D],
                     )
             else:
-                rt = i - MOL_TILES
-                nc.vector.quantize_mx(out=pn_c[:, rt, :].bitcast(FP8X4), scales=pn_s[:, rt, :], in_=g2[:])
+                j = k - MOL_PAIRS
+                nc.vector.quantize_mx(
+                    out=pn_c[:, j, :, :].rearrange("p c m -> p (c m)").bitcast(FP8X4),
+                    scales=pn_s[:, j, :, :].rearrange("p c m -> p (c m)"),
+                    in_=g2[:],
+                )
 
         def similarity(i, engines):
             rt = i - MOL_TILES
+            rows = slice((rt % 2) * P, (rt % 2 + 1) * P)
             osb = work.tile([P, N_MOL], F32, name="osb", tag="osb", bufs=5)
             for nh in range(2):
                 cols = slice(nh * BANK, (nh + 1) * BANK)
@@ -214,8 +217,8 @@ def tile_coembedding_pa_kernel(tc, h_mol, h_prot, Wm2, bm2, Wp2, bp2, temperatur
                 for c in range(2):
                     nc.tensor.matmul_mx(
                         out=bank[:],
-                        lhsT=pn_c[:, rt, c * P:(c + 1) * P].bitcast(FP8X4),
-                        lhsT_scale=pn_s[:, rt, c * P:(c + 1) * P],
+                        lhsT=pn_c[:, rt // 2, c, rows].bitcast(FP8X4),
+                        lhsT_scale=pn_s[:, rt // 2, c, rows],
                         rhs=mn_c[:, c, cols].bitcast(FP8X4),
                         rhs_scale=mn_s[:, c, cols],
                         start=(c == 0),
@@ -227,34 +230,38 @@ def tile_coembedding_pa_kernel(tc, h_mol, h_prot, Wm2, bm2, Wp2, bp2, temperatur
                     nc.scalar.activation(out=osb[:, cols], in_=bank[:], func=ACT.Copy, scale=inv_t[:, 0:1])
             nc.sync.dma_start(out=out[rt * P:(rt + 1) * P, :], in_=osb[:])
 
-        tin = {0: (("hm", 2), ("hm", 3), ("wp", 0)), 1: (("wp", 1), ("wp", 2)), 2: (("wp", 3), ("hp", 0)), 3: (("hp", 1),),
+        tin = {0: (("hm", 3), ("wp", 0)), 1: (("wp", 1), ("wp", 2)), 2: (("wp", 3), ("hp", 0)), 3: (("hp", 1),),
                4: (("hp", 2), ("hp", 3)), 5: (("hp", 4),), 6: (("hp", 5), ("hp", 6)), 7: (("hp", 7),)}
-        warm_up(WARMUPS)
-        transpose_in(("wm", 0), "vs")
-        transpose_in(("wm", 1), "vs")
+        warm_up(4)
+        transpose_in(("wm", 0), "sv")
+        transpose_in(("wm", 1), "sv")
         quantise_in(("wm", 0))
-        transpose_in(("hm", 0), "vs")
+        transpose_in(("hm", 0), "ss")
         quantise_in(("wm", 1))
-        transpose_in(("hm", 1), "vs")
+        transpose_in(("hm", 1), "sv")
         quantise_in(("hm", 0))
-        quantise_in(("hm", 1))
         spread_bias(0)
-        transpose_in(("wm", 2), "vs")
-        transpose_in(("wm", 3), "vs")
-        temperature_reciprocal()
+        project(0, (0,))
+        project(1, (0,))
+        transpose_in(("wm", 2), "ss")
+        quantise_in(("hm", 1))
+        transpose_in(("wm", 3), "ss")
         quantise_in(("wm", 2))
+        project(2, (0,))
+        project(3, (0,))
+        transpose_in(("hm", 2), "ss")
         quantise_in(("wm", 3))
+        temperature_reciprocal()
         for k in range(PAIRS + 4):
             if k < PAIRS:
-                project(2 * k)
-                project(2 * k + 1)
+                project(2 * k, (1,) if k < 2 else (0, 1))
+                project(2 * k + 1, (1,) if k < 2 else (0, 1))
+            if k == 0:
+                quantise_in(("hm", 2))
             for g in tin.get(k - 1, ()):
                 quantise_in(g)
-            if 0 <= k - 1 < PAIRS:
-                clamp(k - 1)
             if 0 <= k - 3 < PAIRS:
-                quantise_rows(2 * (k - 3))
-                quantise_rows(2 * (k - 3) + 1)
+                quantise_rows(k - 3)
             if 0 <= k - 1 < PAIRS:
                 normalise(k - 1)
             if MOL_PAIRS <= k - 4 < PAIRS:

@@ -170,7 +170,7 @@ def tile_coembedding_pa_kernel(tc, h_mol, h_prot, Wm2, bm2, Wp2, bp2, temperatur
 
         def normalise(k):
             rc = work.tile([P, 2], F32, name="rc", tag="rc", bufs=4)
-            nc.gpsimd.tensor_scalar(out=rc[:], in0=rs[k][:], scalar1=1.0 / EPS, scalar2=0.0, op0=ALU.min, op1=ALU.add)
+            nc.vector.tensor_scalar_min(out=rc[:], in0=rs[k][:], scalar1=1.0 / EPS)
             for e in range(2):
                 z = work.tile([P, D], BF16, name="z", tag="z", bufs=6)
                 zs[2 * k + e] = z

@@ -230,34 +230,27 @@ def tile_coembedding_pa_kernel(tc, h_mol, h_prot, Wm2, bm2, Wp2, bp2, temperatur
                     nc.scalar.activation(out=osb[:, cols], in_=bank[:], func=ACT.Copy, scale=inv_t[:, 0:1])
             nc.sync.dma_start(out=out[rt * P:(rt + 1) * P, :], in_=osb[:])
 
-        tin = {0: (("hm", 3), ("wp", 0)), 1: (("wp", 1), ("wp", 2)), 2: (("wp", 3), ("hp", 0)), 3: (("hp", 1),),
+        tin = {0: (("hm", 2), ("hm", 3), ("wp", 0)), 1: (("wp", 1), ("wp", 2)), 2: (("wp", 3), ("hp", 0)), 3: (("hp", 1),),
                4: (("hp", 2), ("hp", 3)), 5: (("hp", 4),), 6: (("hp", 5), ("hp", 6)), 7: (("hp", 7),)}
-        warm_up(4)
-        transpose_in(("wm", 0), "sv")
-        transpose_in(("wm", 1), "sv")
+        warm_up(WARMUPS)
+        transpose_in(("wm", 0), "vs")
+        transpose_in(("wm", 1), "vs")
         quantise_in(("wm", 0))
-        transpose_in(("hm", 0), "ss")
+        transpose_in(("hm", 0), "vs")
         quantise_in(("wm", 1))
-        transpose_in(("hm", 1), "sv")
+        transpose_in(("hm", 1), "vs")
         quantise_in(("hm", 0))
-        spread_bias(0)
-        project(0, (0,))
-        project(1, (0,))
-        transpose_in(("wm", 2), "ss")
         quantise_in(("hm", 1))
-        transpose_in(("wm", 3), "ss")
-        quantise_in(("wm", 2))
-        project(2, (0,))
-        project(3, (0,))
-        transpose_in(("hm", 2), "ss")
-        quantise_in(("wm", 3))
+        spread_bias(0)
+        transpose_in(("wm", 2), "vs")
+        transpose_in(("wm", 3), "vs")
         temperature_reciprocal()
+        quantise_in(("wm", 2))
+        quantise_in(("wm", 3))
         for k in range(PAIRS + 4):
             if k < PAIRS:
-                project(2 * k, (1,) if k < 2 else (0, 1))
-                project(2 * k + 1, (1,) if k < 2 else (0, 1))
-            if k == 0:
-                quantise_in(("hm", 2))
+                project(2 * k)
+                project(2 * k + 1)
             for g in tin.get(k - 1, ()):
                 quantise_in(g)
             if 0 <= k - 3 < PAIRS:

@@ -81,6 +81,7 @@ def tile_coembedding_pa_kernel(tc, h_mol, h_prot, Wm2, bm2, Wp2, bp2, temperatur
         for n in range(8, RAW_BUFS):
             load(n)
         next_load = [RAW_BUFS]
+        tiles_in = [0]
         warm = keep.tile([P, 1], F32, name="warm", tag="warm")
         nc.vector.memset(warm[:], 1.0)
         nc.scalar.activation(out=warm[:], in_=warm[:], func=ACT.Abs_reciprocal_sqrt)
@@ -99,11 +100,13 @@ def tile_coembedding_pa_kernel(tc, h_mol, h_prot, Wm2, bm2, Wp2, bp2, temperatur
             else:
                 nc.scalar.copy(out=out, in_=in_)
 
-        def transpose_in(g, engines):
+        def transpose_in(g):
             grp = work.tile([P, 8 * GROUP], BF16, name="grp", tag="grp", bufs=6, align_bytes=64)
             grouped[g] = grp
             grp_words = grouped[g][:].bitcast(F32).rearrange("q (g n u) -> q g n u", g=2, n=GROUP, u=2)
-            for t, engine in enumerate(engines):
+            for t in range(2):
+                engine = "v" if tiles_in[0] % 3 == 0 else "s"
+                tiles_in[0] += 1
                 words = raws[g, t][:].bitcast(F32)
                 bank = psum.tile([P, 4, P], F32, name="tin", tag="bank")
                 for gu in range(4):
@@ -228,40 +231,43 @@ def tile_coembedding_pa_kernel(tc, h_mol, h_prot, Wm2, bm2, Wp2, bp2, temperatur
                     nc.vector.tensor_scalar_mul(out=osb[:, cols], in0=bank[:], scalar1=inv_t[:, 0:1])
                 else:
                     nc.scalar.activation(out=osb[:, cols], in_=bank[:], func=ACT.Copy, scale=inv_t[:, 0:1])
-            nc.sync.dma_start(out=out[rt * P:(rt + 1) * P, :], in_=osb[:])
+                nc.sync.dma_start(out=out[rt * P:(rt + 1) * P, cols], in_=osb[:, cols])
 
-        tin = {0: (("hm", 2), ("hm", 3), ("wp", 0)), 1: (("wp", 1), ("wp", 2)), 2: (("wp", 3), ("hp", 0)), 3: (("hp", 1),),
+        tin = {0: (("hm", 3), ("wp", 0), ("wp", 1)), 1: (("wp", 2), ("wp", 3)), 2: (("hp", 0),), 3: (("hp", 1),),
                4: (("hp", 2), ("hp", 3)), 5: (("hp", 4),), 6: (("hp", 5), ("hp", 6)), 7: (("hp", 7),)}
-        warm_up(WARMUPS)
-        transpose_in(("wm", 0), "vs")
-        transpose_in(("wm", 1), "vs")
+        warm_up(8)
+        transpose_in(("wm", 0))
+        transpose_in(("wm", 1))
         quantise_in(("wm", 0))
-        transpose_in(("hm", 0), "vs")
+        transpose_in(("hm", 0))
         quantise_in(("wm", 1))
-        transpose_in(("hm", 1), "vs")
+        transpose_in(("hm", 1))
         quantise_in(("hm", 0))
-        quantise_in(("hm", 1))
         spread_bias(0)
-        transpose_in(("wm", 2), "vs")
-        transpose_in(("wm", 3), "vs")
-        temperature_reciprocal()
+        transpose_in(("wm", 2))
+        quantise_in(("hm", 1))
+        transpose_in(("wm", 3))
         quantise_in(("wm", 2))
+        transpose_in(("hm", 2))
         quantise_in(("wm", 3))
+        temperature_reciprocal()
         for k in range(PAIRS + 4):
             if k < PAIRS:
                 project(2 * k)
                 project(2 * k + 1)
+            if k == 0:
+                quantise_in(("hm", 2))
             for g in tin.get(k - 1, ()):
                 quantise_in(g)
             if 0 <= k - 3 < PAIRS:
                 quantise_rows(k - 3)
-            if 0 <= k - 1 < PAIRS:
-                normalise(k - 1)
             if MOL_PAIRS <= k - 4 < PAIRS:
                 for i in (2 * (k - 4), 2 * (k - 4) + 1):
-                    similarity(i, "sv" if i % 3 == 1 else "ss")
+                    similarity(i, "sv" if i % 2 == 1 else "ss")
+            if 0 <= k - 1 < PAIRS:
+                normalise(k - 1)
             for g in tin.get(k, ()):
-                transpose_in(g, "sv" if g[1] % 2 == 1 else "ss")
+                transpose_in(g)
             if 0 <= k - 2 < PAIRS:
                 for i in (2 * (k - 2), 2 * (k - 2) + 1):
                     transpose_rows(i, "v" if i >= 12 or i % 4 == 3 else "s")

@@ -56,7 +56,7 @@ def tile_coembedding_pa_kernel(tc, h_mol, h_prot, Wm2, bm2, Wp2, bp2, temperatur
         load_order += [("wp", j) for j in range(4)]
         load_order += [("hp", j) for j in range(8)]
         load_order = [(g, t) for g in load_order for t in range(2)]
-        raws, grouped, biases, ys, rs, zs, regrouped = {}, {}, {}, {}, {}, {}, {}
+        raws, grouped, ys, sums, rs, zs, regrouped = {}, {}, {}, {}, {}, {}, {}
 
         def load(n):
             if n < len(load_order):
@@ -66,7 +66,8 @@ def tile_coembedding_pa_kernel(tc, h_mol, h_prot, Wm2, bm2, Wp2, bp2, temperatur
                 raws[g, t] = raw
                 nc.sync.dma_start(out=raw[:], in_=src[row0:row0 + P, :])
 
-        brow = keep.tile([P, 2 * D], BF16, name="brow", tag="brow")
+        brow = keep.tile([P, D], BF16, name="brow", tag="brow")
+        bias_p = keep.tile([P, D], BF16, name="bias_p", tag="bias_p")
         ones_b = keep.tile([P, P], BF16, name="ones_b", tag="ones_b")
         nc.vector.memset(ones_b[:], 1.0)
         zeros_b = keep.tile([P, BANK], BF16, name="zeros_b", tag="zeros_b")
@@ -77,11 +78,12 @@ def tile_coembedding_pa_kernel(tc, h_mol, h_prot, Wm2, bm2, Wp2, bp2, temperatur
         for n in range(8):
             load(n)
         nc.sync.dma_start(out=brow[0:1, 0:D], in_=bm2.rearrange("(o n) -> o n", o=1))
-        nc.sync.dma_start(out=brow[0:1, D:2 * D], in_=bp2.rearrange("(o n) -> o n", o=1))
         for n in range(8, RAW_BUFS):
             load(n)
+        nc.sync.dma_start(out=bias_p[:], in_=bp2.partition_broadcast(P))
         next_load = [RAW_BUFS]
         tiles_in = [0]
+        bias_m = keep.tile([P, D], F32, name="bias_m", tag="bias_m")
         warm = keep.tile([P, 1], F32, name="warm", tag="warm")
         nc.vector.memset(warm[:], 1.0)
         nc.scalar.activation(out=warm[:], in_=warm[:], func=ACT.Abs_reciprocal_sqrt)
@@ -105,7 +107,7 @@ def tile_coembedding_pa_kernel(tc, h_mol, h_prot, Wm2, bm2, Wp2, bp2, temperatur
             grouped[g] = grp
             grp_words = grouped[g][:].bitcast(F32).rearrange("q (g n u) -> q g n u", g=2, n=GROUP, u=2)
             for t in range(2):
-                engine = "v" if tiles_in[0] % 3 == 0 else "s"
+                engine = "v" if (tiles_in[0] % 3 == 0) else "s"
                 tiles_in[0] += 1
                 words = raws[g, t][:].bitcast(F32)
                 bank = psum.tile([P, 4, P], F32, name="tin", tag="bank")
@@ -129,25 +131,22 @@ def tile_coembedding_pa_kernel(tc, h_mol, h_prot, Wm2, bm2, Wp2, bp2, temperatur
             for m in range(n):
                 nc.tensor.matmul(bank[:], lhsT=ones_b[:], rhs=zeros_b[:], start=True, stop=True)
 
-        def spread_bias(b):
-            bias = keep.tile([P, D], F32, name="bias%d" % b, tag="bias%d" % b)
-            biases[b] = bias
+        def spread_bias():
             for c in range(2):
+                cols = slice(c * BANK, (c + 1) * BANK)
                 bank = psum.tile([P, BANK], F32, name="bb", tag="bank")
-                lo = b * D + c * BANK
-                nc.tensor.matmul(bank[:], lhsT=ones_b[:], rhs=brow[:, lo:lo + BANK], start=True, stop=True)
-                nc.scalar.copy(out=bias[:, c * BANK:(c + 1) * BANK], in_=bank[:])
+                nc.tensor.matmul(bank[:], lhsT=ones_b[:], rhs=brow[:, cols], start=True, stop=True)
+                nc.scalar.copy(out=bias_m[:, cols], in_=bank[:])
 
-        def project(i, halves=(0, 1)):
+        def project(i):
             if i < MOL_TILES:
-                hc, hs, wc, ws, bias, rows = hm_c, hm_s, wm_c, wm_s, biases[0], slice(i * P, (i + 1) * P)
+                hc, hs, wc, ws, bias, rows = hm_c, hm_s, wm_c, wm_s, bias_m, slice(i * P, (i + 1) * P)
             else:
-                hc, hs, wc, ws, bias = hp_c, hp_s, wp_c, wp_s, biases[1]
+                hc, hs, wc, ws, bias = hp_c, hp_s, wp_c, wp_s, bias_p
                 rows = slice((i - MOL_TILES) * P, (i - MOL_TILES + 1) * P)
-            if i not in ys:
-                y = work.tile([P, D], F32, name="y", tag="y", bufs=6)
-                ys[i] = y
-            for c in halves:
+            y = work.tile([P, D], F32, name="y", tag="y", bufs=6)
+            ys[i] = y
+            for c in range(2):
                 cols = slice(c * BANK, (c + 1) * BANK)
                 bank = psum.tile([P, BANK], F32, name="x", tag="bank")
                 for p in range(2):
@@ -160,16 +159,19 @@ def tile_coembedding_pa_kernel(tc, h_mol, h_prot, Wm2, bm2, Wp2, bp2, temperatur
                         start=(p == 0),
                         stop=(p == 1),
                     )
-                nc.vector.tensor_tensor(out=ys[i][:, cols], in0=bank[:], in1=bias[:, cols], op=ALU.add)
+                nc.vector.tensor_tensor(out=y[:, cols], in0=bank[:], in1=bias[:, cols], op=ALU.add)
 
-        def row_norms(k):
-            ss = work.tile([P, 2], F32, name="ss", tag="ss", bufs=4)
-            for e in range(2):
-                squares = work.tile([P, D], BF16, name="squares", tag="squares", bufs=1)
-                nc.scalar.activation(out=squares[:], in_=ys[2 * k + e][:], func=ACT.Square, accum_out=ss[:, e:e + 1])
-            r = work.tile([P, 2], F32, name="r", tag="r", bufs=4)
-            nc.scalar.activation(out=r[:], in_=ss[:], func=ACT.Abs_reciprocal_sqrt)
-            rs[k] = r
+        def square_sum(i):
+            k, e = i // 2, i % 2
+            if e == 0:
+                ss = work.tile([P, 2], F32, name="ss", tag="ss", bufs=4)
+                sums[k] = ss
+            squares = work.tile([P, D], BF16, name="squares", tag="squares", bufs=1)
+            nc.scalar.activation(out=squares[:], in_=ys[i][:], func=ACT.Square, accum_out=sums[k][:, e:e + 1])
+            if e == 1:
+                r = work.tile([P, 2], F32, name="r", tag="r", bufs=4)
+                nc.scalar.activation(out=r[:], in_=sums[k][:], func=ACT.Abs_reciprocal_sqrt)
+                rs[k] = r
 
         def normalise(k):
             rc = work.tile([P, 2], F32, name="rc", tag="rc", bufs=4)
@@ -233,7 +235,7 @@ def tile_coembedding_pa_kernel(tc, h_mol, h_prot, Wm2, bm2, Wp2, bp2, temperatur
                     nc.scalar.activation(out=osb[:, cols], in_=bank[:], func=ACT.Copy, scale=inv_t[:, 0:1])
                 nc.sync.dma_start(out=out[rt * P:(rt + 1) * P, cols], in_=osb[:, cols])
 
-        tin = {0: (("hm", 3), ("wp", 0), ("wp", 1)), 1: (("wp", 2), ("wp", 3)), 2: (("hp", 0),), 3: (("hp", 1),),
+        tin = {0: (("hm", 3), ("wp", 0)), 1: (("wp", 1), ("wp", 2), ("wp", 3)), 2: (("hp", 0),), 3: (("hp", 1),),
                4: (("hp", 2), ("hp", 3)), 5: (("hp", 4),), 6: (("hp", 5), ("hp", 6)), 7: (("hp", 7),)}
         warm_up(8)
         transpose_in(("wm", 0))
@@ -243,7 +245,7 @@ def tile_coembedding_pa_kernel(tc, h_mol, h_prot, Wm2, bm2, Wp2, bp2, temperatur
         quantise_in(("wm", 1))
         transpose_in(("hm", 1))
         quantise_in(("hm", 0))
-        spread_bias(0)
+        spread_bias()
         transpose_in(("wm", 2))
         quantise_in(("hm", 1))
         transpose_in(("wm", 3))
@@ -252,26 +254,36 @@ def tile_coembedding_pa_kernel(tc, h_mol, h_prot, Wm2, bm2, Wp2, bp2, temperatur
         quantise_in(("wm", 3))
         temperature_reciprocal()
         for k in range(PAIRS + 4):
+            new = tin.get(k, ())
+            half = (len(new) + 1) // 2
             if k < PAIRS:
                 project(2 * k)
-                project(2 * k + 1)
+            if 0 <= k - 3 < PAIRS:
+                quantise_rows(k - 3)
             if k == 0:
                 quantise_in(("hm", 2))
             for g in tin.get(k - 1, ()):
                 quantise_in(g)
-            if 0 <= k - 3 < PAIRS:
-                quantise_rows(k - 3)
             if MOL_PAIRS <= k - 4 < PAIRS:
-                for i in (2 * (k - 4), 2 * (k - 4) + 1):
-                    similarity(i, "sv" if i % 2 == 1 else "ss")
+                i = 2 * (k - 4)
+                similarity(i, "sv" if i % 2 == 1 else "ss")
             if 0 <= k - 1 < PAIRS:
                 normalise(k - 1)
-            for g in tin.get(k, ()):
+            for g in new[:half]:
+                transpose_in(g)
+            if MOL_PAIRS <= k - 4 < PAIRS:
+                i = 2 * (k - 4) + 1
+                similarity(i, "sv" if i % 2 == 1 else "ss")
+            if k < PAIRS:
+                square_sum(2 * k)
+                project(2 * k + 1)
+            if 0 <= k - 2 < PAIRS:
+                i = 2 * (k - 2)
+                transpose_rows(i, "v" if i >= 12 or i % 4 == 3 else "s")
+            for g in new[half:]:
                 transpose_in(g)
             if 0 <= k - 2 < PAIRS:
-                for i in (2 * (k - 2), 2 * (k - 2) + 1):
-                    transpose_rows(i, "v" if i >= 12 or i % 4 == 3 else "s")
+                i = 2 * (k - 2) + 1
+                transpose_rows(i, "v" if i >= 12 or i % 4 == 3 else "s")
             if k < PAIRS:
-                row_norms(k)
-            if k == 0:
-                spread_bias(1)
+                square_sum(2 * k + 1)

@@ -35,8 +35,15 @@ def tile_coembedding_pa_kernel(tc, h_mol, h_prot, Wm2, bm2, Wp2, bp2, temperatur
         ctx.enter_context(tc.manual_schedule())
 
         def codes_and_scales(label, shape):
-            codes = keep.tile(shape, U32, name=label + "_c", tag=label + "_c", align_bytes=64)
-            scales = keep.tile(shape, U8, name=label + "_s", tag=label + "_s", align_bytes=64)
+            codes = keep.tile(shape, U32, name=label + "_c", tag=label + "_c", align_bytes=256)
+            size = 1
+            for n in shape[1:]:
+                size *= n
+            room = keep.tile([P, 64 + size], U8, name=label + "_s", tag=label + "_s", align_bytes=256)
+            if len(shape) == 3:
+                scales = room[:, 64:].rearrange("p (a n) -> p a n", a=shape[1])
+            else:
+                scales = room[:, 64:].rearrange("p (a b n) -> p a b n", a=shape[1], b=shape[2])
             return codes, scales
 
         wm_c, wm_s = codes_and_scales("wm", [P, 2, D])

from contextlib import ExitStack

import concourse.masks as masks
import concourse.mybir as mybir

F32 = mybir.dt.float32
BF16 = mybir.dt.bfloat16
U32 = mybir.dt.uint32
U8 = mybir.dt.uint8
FP8X4 = mybir.dt.float8_e4m3fn_x4
ACT = mybir.ActivationFunctionType
ALU = mybir.AluOpType

P = 128
N_MOL, N_PROT, F, D = 1024, 2048, 1024, 1024
EPS = 1e-8
FLOPS = 2 * (N_MOL * F * D + N_PROT * F * D + N_PROT * N_MOL * D)

BANK = 512
GROUP = 2 * P
MOL_TILES = N_MOL // P
TILES = (N_MOL + N_PROT) // P
PAIRS = TILES // 2
MOL_PAIRS = MOL_TILES // 2
RAW_BUFS = 24
WARMUPS = 8


def tile_coembedding_pa_kernel(tc, h_mol, h_prot, Wm2, bm2, Wp2, bp2, temperature, out):
    nc = tc.nc
    with ExitStack() as ctx:
        keep = ctx.enter_context(tc.tile_pool(name="keep", bufs=1))
        work = ctx.enter_context(tc.tile_pool(name="work", bufs=1))
        psum = ctx.enter_context(tc.psum_pool(name="psum", bufs=8))
        ctx.enter_context(tc.manual_schedule())

        def codes_and_scales(label, shape):
            codes = keep.tile(shape, U32, name=label + "_c", tag=label + "_c", align_bytes=256)
            size = 1
            for n in shape[1:]:
                size *= n
            room = keep.tile([P, 64 + size], U8, name=label + "_s", tag=label + "_s", align_bytes=256)
            if len(shape) == 3:
                scales = room[:, 64:].rearrange("p (a n) -> p a n", a=shape[1])
            else:
                scales = room[:, 64:].rearrange("p (a b n) -> p a b n", a=shape[1], b=shape[2])
            return codes, scales

        wm_c, wm_s = codes_and_scales("wm", [P, 2, D])
        wp_c, wp_s = codes_and_scales("wp", [P, 2, D])
        hm_c, hm_s = codes_and_scales("hm", [P, 2, N_MOL])
        hp_c, hp_s = codes_and_scales("hp", [P, 2, N_PROT])
        mn_c, mn_s = codes_and_scales("mn", [P, 2, N_MOL])
        pn_c, pn_s = codes_and_scales("pn", [P, N_PROT // GROUP, 2, GROUP])

        groups = {}
        for label, src, codes, scales, n in (
            ("wm", Wm2, wm_c, wm_s, 4), ("hm", h_mol, hm_c, hm_s, 4), ("wp", Wp2, wp_c, wp_s, 4), ("hp", h_prot, hp_c, hp_s, 8),
        ):
            for j in range(n):
                groups[label, j] = (src, j * GROUP, codes, scales)
        load_order = [("wm", 0), ("wm", 1), ("hm", 0), ("hm", 1), ("wm", 2), ("wm", 3), ("hm", 2), ("hm", 3)]
        load_order += [("wp", j) for j in range(4)]
        load_order += [("hp", j) for j in range(8)]
        load_order = [(g, t) for g in load_order for t in range(2)]
        raws, grouped, ys, sums, rs, zs, regrouped = {}, {}, {}, {}, {}, {}, {}

        def load(n):
            if n < len(load_order):
                g, t = load_order[n]
                src, row0 = groups[g][0], groups[g][1] + t * P
                raw = work.tile([P, F], BF16, name="raw", tag="raw", bufs=RAW_BUFS)
                raws[g, t] = raw
                nc.sync.dma_start(out=raw[:], in_=src[row0:row0 + P, :])

        brow = keep.tile([P, D], BF16, name="brow", tag="brow")
        bias_p = keep.tile([P, D], BF16, name="bias_p", tag="bias_p")
        ones_b = keep.tile([P, P], BF16, name="ones_b", tag="ones_b")
        nc.vector.memset(ones_b[:], 1.0)
        zeros_b = keep.tile([P, BANK], BF16, name="zeros_b", tag="zeros_b")
        nc.vector.memset(zeros_b[:], 0.0)
        nc.vector.memset(brow[:], 0.0)
        t_bf = keep.tile([P, 1], BF16, name="t_bf", tag="t_bf")
        nc.scalar.dma_start(out=t_bf[:], in_=temperature.partition_broadcast(P))
        for n in range(8):
            load(n)
        nc.sync.dma_start(out=brow[0:1, 0:D], in_=bm2.rearrange("(o n) -> o n", o=1))
        for n in range(8, RAW_BUFS):
            load(n)
        nc.sync.dma_start(out=bias_p[:], in_=bp2.partition_broadcast(P))
        next_load = [RAW_BUFS]
        tiles_in = [0]
        bias_m = keep.tile([P, D], F32, name="bias_m", tag="bias_m")
        warm = keep.tile([P, 1], F32, name="warm", tag="warm")
        nc.vector.memset(warm[:], 1.0)
        nc.scalar.activation(out=warm[:], in_=warm[:], func=ACT.Abs_reciprocal_sqrt)
        ident_f = keep.tile([P, P], F32, name="ident_f", tag="ident_f")
        masks.make_identity(nc, ident_f[:])
        t_f = keep.tile([P, 1], F32, name="t_f", tag="t_f")
        inv_t = keep.tile([P, 1], F32, name="inv_t", tag="inv_t")

        def temperature_reciprocal():
            nc.vector.tensor_copy(out=t_f[:], in_=t_bf[:])
            nc.vector.reciprocal(out=inv_t[:], in_=t_f[:])

        def copy_out(engine, out, in_):
            if engine == "v":
                nc.vector.tensor_copy(out=out, in_=in_)
            else:
                nc.scalar.copy(out=out, in_=in_)

        def transpose_in(g):
            grp = work.tile([P, 8 * GROUP], BF16, name="grp", tag="grp", bufs=6, align_bytes=64)
            grouped[g] = grp
            grp_words = grouped[g][:].bitcast(F32).rearrange("q (g n u) -> q g n u", g=2, n=GROUP, u=2)
            for t in range(2):
                engine = "v" if (tiles_in[0] % 3 == 0) else "s"
                tiles_in[0] += 1
                words = raws[g, t][:].bitcast(F32)
                bank = psum.tile([P, 4, P], F32, name="tin", tag="bank")
                for gu in range(4):
                    nc.tensor.transpose(bank[:, gu, :], words[:, gu * P:(gu + 1) * P], ident_f[:])
                copy_out(engine, grp_words[:, :, t * P:(t + 1) * P, :], bank[:].rearrange("q (g u) r -> q g r u", g=2, u=2))
                load(next_load[0])
                next_load[0] += 1

        def quantise_in(g):
            codes, scales, col0 = groups[g][2], groups[g][3], groups[g][1]
            for p in range(2):
                nc.vector.quantize_mx(
                    out=codes[:, p, col0:col0 + GROUP].bitcast(FP8X4),
                    scales=scales[:, p, col0:col0 + GROUP],
                    in_=grouped[g][:, p * 4 * GROUP:(p + 1) * 4 * GROUP],
                )

        def warm_up(n):
            bank = psum.tile([P, BANK], F32, name="wu", tag="bank")
            for m in range(n):
                nc.tensor.matmul(bank[:], lhsT=ones_b[:], rhs=zeros_b[:], start=True, stop=True)

        def spread_bias():
            for c in range(2):
                cols = slice(c * BANK, (c + 1) * BANK)
                bank = psum.tile([P, BANK], F32, name="bb", tag="bank")
                nc.tensor.matmul(bank[:], lhsT=ones_b[:], rhs=brow[:, cols], start=True, stop=True)
                nc.scalar.copy(out=bias_m[:, cols], in_=bank[:])

        def project(i):
            if i < MOL_TILES:
                hc, hs, wc, ws, bias, rows = hm_c, hm_s, wm_c, wm_s, bias_m, slice(i * P, (i + 1) * P)
            else:
                hc, hs, wc, ws, bias = hp_c, hp_s, wp_c, wp_s, bias_p
                rows = slice((i - MOL_TILES) * P, (i - MOL_TILES + 1) * P)
            y = work.tile([P, D], F32, name="y", tag="y", bufs=6)
            ys[i] = y
            for c in range(2):
                cols = slice(c * BANK, (c + 1) * BANK)
                bank = psum.tile([P, BANK], F32, name="x", tag="bank")
                for p in range(2):
                    nc.tensor.matmul_mx(
                        out=bank[:],
                        lhsT=hc[:, p, rows].bitcast(FP8X4),
                        lhsT_scale=hs[:, p, rows],
                        rhs=wc[:, p, cols].bitcast(FP8X4),
                        rhs_scale=ws[:, p, cols],
                        start=(p == 0),
                        stop=(p == 1),
                    )
                nc.vector.tensor_tensor(out=y[:, cols], in0=bank[:], in1=bias[:, cols], op=ALU.add)

        def square_sum(i):
            k, e = i // 2, i % 2
            if e == 0:
                ss = work.tile([P, 2], F32, name="ss", tag="ss", bufs=4)
                sums[k] = ss
            squares = work.tile([P, D], BF16, name="squares", tag="squares", bufs=1)
            nc.scalar.activation(out=squares[:], in_=ys[i][:], func=ACT.Square, accum_out=sums[k][:, e:e + 1])
            if e == 1:
                r = work.tile([P, 2], F32, name="r", tag="r", bufs=4)
                nc.scalar.activation(out=r[:], in_=sums[k][:], func=ACT.Abs_reciprocal_sqrt)
                rs[k] = r

        def normalise(k):
            rc = work.tile([P, 2], F32, name="rc", tag="rc", bufs=4)
            nc.vector.tensor_scalar_min(out=rc[:], in0=rs[k][:], scalar1=1.0 / EPS)
            for e in range(2):
                z = work.tile([P, D], BF16, name="z", tag="z", bufs=6)
                zs[2 * k + e] = z
                nc.gpsimd.tensor_scalar(
                    out=z[:], in0=ys[2 * k + e][:], scalar1=rc[:, e:e + 1], scalar2=0.0, op0=ALU.mult, op1=ALU.add
                )

        def transpose_rows(i, engine):
            words = zs[i][:].bitcast(F32)
            bank = psum.tile([P, 4, P], F32, name="t2", tag="bank")
            for cu in range(4):
                nc.tensor.transpose(bank[:, cu, :], words[:, cu * P:(cu + 1) * P], ident_f[:])
            if i % 2 == 0:
                g2 = work.tile([P, 2 * D], BF16, name="g2", tag="g2", bufs=3, align_bytes=64)
                regrouped[i // 2] = g2
            dst = regrouped[i // 2][:].bitcast(F32).rearrange("p (c m u) -> p c m u", c=2, m=2 * P, u=2)
            lo = (i % 2) * P
            copy_out(engine, dst[:, :, lo:lo + P, :], bank[:].rearrange("p (c u) m -> p c m u", c=2, u=2))

        def quantise_rows(k):
            g2 = regrouped[k]
            if k < MOL_PAIRS:
                for c in range(2):
                    nc.vector.quantize_mx(
                        out=mn_c[:, c, 2 * k * P:2 * (k + 1) * P].bitcast(FP8X4),
                        scales=mn_s[:, c, 2 * k * P:2 * (k + 1) * P],
                        in_=g2[:, c * D:(c + 1) * D],
                    )
            else:
                j = k - MOL_PAIRS
                nc.vector.quantize_mx(
                    out=pn_c[:, j, :, :].rearrange("p c m -> p (c m)").bitcast(FP8X4),
                    scales=pn_s[:, j, :, :].rearrange("p c m -> p (c m)"),
                    in_=g2[:],
                )

        def similarity(i, engines):
            rt = i - MOL_TILES
            rows = slice((rt % 2) * P, (rt % 2 + 1) * P)
            osb = work.tile([P, N_MOL], F32, name="osb", tag="osb", bufs=5)
            for nh in range(2):
                cols = slice(nh * BANK, (nh + 1) * BANK)
                bank = psum.tile([P, BANK], F32, name="o", tag="bank")
                for c in range(2):
                    nc.tensor.matmul_mx(
                        out=bank[:],
                        lhsT=pn_c[:, rt // 2, c, rows].bitcast(FP8X4),
                        lhsT_scale=pn_s[:, rt // 2, c, rows],
                        rhs=mn_c[:, c, cols].bitcast(FP8X4),
                        rhs_scale=mn_s[:, c, cols],
                        start=(c == 0),
                        stop=(c == 1),
                    )
                if engines[nh] == "v":
                    nc.vector.tensor_scalar_mul(out=osb[:, cols], in0=bank[:], scalar1=inv_t[:, 0:1])
                else:
                    nc.scalar.activation(out=osb[:, cols], in_=bank[:], func=ACT.Copy, scale=inv_t[:, 0:1])
                nc.sync.dma_start(out=out[rt * P:(rt + 1) * P, cols], in_=osb[:, cols])

        tin = {0: (("hm", 3), ("wp", 0)), 1: (("wp", 1), ("wp", 2), ("wp", 3)), 2: (("hp", 0),), 3: (("hp", 1),),
               4: (("hp", 2), ("hp", 3)), 5: (("hp", 4),), 6: (("hp", 5), ("hp", 6)), 7: (("hp", 7),)}
        warm_up(8)
        transpose_in(("wm", 0))
        transpose_in(("wm", 1))
        quantise_in(("wm", 0))
        transpose_in(("hm", 0))
        quantise_in(("wm", 1))
        transpose_in(("hm", 1))
        quantise_in(("hm", 0))
        spread_bias()
        transpose_in(("wm", 2))
        quantise_in(("hm", 1))
        transpose_in(("wm", 3))
        quantise_in(("wm", 2))
        transpose_in(("hm", 2))
        quantise_in(("wm", 3))
        temperature_reciprocal()
        for k in range(PAIRS + 4):
            new = tin.get(k, ())
            half = (len(new) + 1) // 2
            if k < PAIRS:
                project(2 * k)
            if 0 <= k - 3 < PAIRS:
                quantise_rows(k - 3)
            if k == 0:
                quantise_in(("hm", 2))
            for g in tin.get(k - 1, ()):
                quantise_in(g)
            if MOL_PAIRS <= k - 4 < PAIRS:
                i = 2 * (k - 4)
                similarity(i, "sv" if i % 2 == 1 else "ss")
            if 0 <= k - 1 < PAIRS:
                normalise(k - 1)
            for g in new[:half]:
                transpose_in(g)
            if MOL_PAIRS <= k - 4 < PAIRS:
                i = 2 * (k - 4) + 1
                similarity(i, "sv" if i % 2 == 1 else "ss")
            if k < PAIRS:
                square_sum(2 * k)
                project(2 * k + 1)
            if 0 <= k - 2 < PAIRS:
                i = 2 * (k - 2)
                transpose_rows(i, "v" if i >= 12 or i % 4 == 3 else "s")
            for g in new[half:]:
                transpose_in(g)
            if 0 <= k - 2 < PAIRS:
                i = 2 * (k - 2) + 1
                transpose_rows(i, "v" if i >= 12 or i % 4 == 3 else "s")
            if k < PAIRS:
                square_sum(2 * k + 1)
